import numpy as np
import ml_dtypes


def mxq(x, axis, fmt="e4m3"):
    dtype, down = {"e4m3": (ml_dtypes.float8_e4m3fn, 7), "e5m2": (ml_dtypes.float8_e5m2, 14)}[fmt]
    v = np.moveaxis(np.asarray(x, np.float32).astype(ml_dtypes.bfloat16).astype(np.float64), axis, -1)
    blocks = v.reshape(v.shape[:-1] + (-1, 32))
    amax = np.abs(blocks).max(-1, keepdims=True)
    byte = np.maximum(np.where(amax > 0, np.frexp(amax)[1] - 1 + 127, 0) - down, 1)
    scale = np.exp2(byte - 127.0)
    codes = (blocks / scale).astype(np.float32).astype(dtype).astype(np.float64)
    return np.moveaxis((codes * scale).reshape(v.shape), -1, axis)


WIDE = False


def mx_kscale(k):
    if not WIDE:
        return np.ones(k)
    levels = np.array([10, -10, 5, -5, 0])
    a = np.random.permutation(np.resize(levels, k // 512 * 4)).reshape(k // 512, 4)
    idx = np.arange(k)
    return np.exp2(a[idx // 512, idx % 128 // 32])


BF16 = ml_dtypes.bfloat16


def bf(x):
    return np.asarray(x, np.float32).astype(BF16)


def f64(x):
    return np.asarray(x).astype(np.float64)


N, KZ, C, M0, M1, M2 = 2048, 16, 4, 128, 64, 32
MULS = (M0, M1, M2)
LS = (0, 1, 2)


def setup_inputs():
    xs, ws = [], []
    for m, l in zip(MULS, LS):
        d = 2 * l + 1
        a = mx_kscale(m * KZ)[::KZ]
        xs.append((np.random.standard_normal((N, m, d)) * a[None, :, None]).reshape(N, m * d))
        ws.append(np.random.standard_normal((m, KZ, C * m)) * (m * KZ) ** -0.25 / a[:, None, None])
    z = np.random.standard_normal((N, KZ))
    return {"node_embeddings": bf(np.concatenate(xs, axis=1)), "Z_embeddings": bf(z),
            "W0": bf(ws[0]), "W1": bf(ws[1]), "W2": bf(ws[2])}


def reference(node_embeddings, Z_embeddings, W0, W1, W2):
    x, z = f64(node_embeddings), f64(Z_embeddings)
    outs = []
    off = 0
    for m, l, W in zip(MULS, LS, (W0, W1, W2)):
        d = 2 * l + 1
        x_l = x[:, off:off + m * d].reshape(-1, m, d)
        off += m * d
        alpha = 1.0 / np.sqrt(m * KZ)
        p = (x_l.transpose(0, 2, 1)[:, :, :, None] * z[:, None, None, :]).reshape(-1, d, m * KZ)
        o = (mxq(p, 2, "e4m3") @ mxq(f64(W).reshape(m * KZ, C * m), 0, "e4m3")) * alpha
        outs.append(o.transpose(0, 2, 1).reshape(-1, m * d))
    return np.concatenate(outs, axis=-1)

@@ -1,0 +1,316 @@
+import math
+from contextlib import ExitStack
+
+import concourse.mybir as mybir
+from concourse.masks import make_identity
+
+BF16 = mybir.dt.bfloat16
+F32 = mybir.dt.float32
+U32 = mybir.dt.uint32
+U8 = mybir.dt.uint8
+I32 = mybir.dt.int32
+FP8X4 = mybir.dt.float8_e4m3fn_x4
+COPY = mybir.ActivationFunctionType.Copy
+MULT = mybir.AluOpType.mult
+
+P = 128
+NODES = 2048
+NJ = NODES // P
+FEAT = 480
+FLOPS = 2 * NODES * (1 * 2048 * 512 + 3 * 1024 * 256 + 5 * 512 * 128)
+
+ALPHA0 = 1.0 / math.sqrt(2048.0)
+ALPHA1 = 1.0 / math.sqrt(1024.0)
+ALPHA2 = 1.0 / math.sqrt(512.0)
+
+
+def tile_tensorproductselfinteraction_kernel(tc, node_embeddings, Z_embeddings, W0, W1, W2, out):
+    nc = tc.nc
+    x_view = node_embeddings.rearrange("(j q) f -> q j f", q=P)
+    z_view = Z_embeddings.rearrange("(k n) v -> k (n v)", k=NJ // 2)
+    out_view = out.rearrange("(j q c) f -> j q (c f)", q=P, c=4)
+
+    with ExitStack() as ctx:
+        const = ctx.enter_context(tc.tile_pool(name="const", bufs=1))
+        zpool = ctx.enter_context(tc.tile_pool(name="zpool", bufs=3))
+        xtpool = ctx.enter_context(tc.tile_pool(name="xtpool", bufs=3))
+        ppool = ctx.enter_context(tc.tile_pool(name="ppool", bufs=3))
+        wgpool = ctx.enter_context(tc.tile_pool(name="wgpool", bufs=2))
+        cpool = ctx.enter_context(tc.tile_pool(name="cpool", bufs=4))
+        opool = ctx.enter_context(tc.tile_pool(name="opool", bufs=3))
+        ps_t = ctx.enter_context(tc.psum_pool(name="ps_t", bufs=3))
+        ps_o = ctx.enter_context(tc.psum_pool(name="ps_o", bufs=1))
+
+        ident = const.tile([P, P], BF16, name="ident")
+        make_identity(nc, ident[:])
+        sel0 = const.tile([P, P], BF16, name="sel0")
+        sel1 = const.tile([P, P], BF16, name="sel1")
+        sel2 = const.tile([P, P], BF16, name="sel2")
+
+        w0c = const.tile([P, 4, 512], U32, name="w0c", align_bytes=64)
+        w0s = const.tile([P, 4, 512], U8, name="w0s", align_bytes=64)
+        c1 = const.tile([P, 8, 128], U32, name="c1", align_bytes=64)
+        s1 = const.tile([P, 8, 128], U8, name="s1", align_bytes=64)
+        c2 = const.tile([P, 8, 64], U32, name="c2", align_bytes=64)
+        s2 = const.tile([P, 8, 64], U8, name="s2", align_bytes=64)
+        m1 = const.tile([P, 8, 256], U32, name="m1", align_bytes=64)
+        sm1 = const.tile([P, 8, 256], U8, name="sm1", align_bytes=64)
+        m2 = const.tile([P, 8, 256], U32, name="m2", align_bytes=64)
+        sm2 = const.tile([P, 8, 256], U8, name="sm2", align_bytes=64)
+
+        wraw0 = const.tile([P, 16, 512], BF16, name="wraw0")
+        wraw1 = const.tile([P, 16, 256], BF16, name="wraw1")
+        wraw2 = const.tile([P, 16, 128], BF16, name="wraw2")
+        xn = [const.tile([P, 4, FEAT], BF16, name="xn%d" % c) for c in range(4)]
+        xa = [const.tile([P, 512], BF16, name="xa%d" % k) for k in range(4)]
+
+        nc.vector.memset(m1[:].bitcast(I32), 0)
+        nc.vector.memset(m2[:].bitcast(I32), 0)
+        nc.vector.memset(s1[:].bitcast(I32), 0)
+        nc.vector.memset(s2[:].bitcast(I32), 0)
+        nc.vector.memset(wraw1[64:128, :, :].bitcast(I32), 0)
+        nc.vector.memset(wraw2[:].bitcast(I32), 0)
+        for k in range(4):
+            nc.vector.memset(xa[k][:, FEAT:512].bitcast(I32), 0)
+
+        zb = {}
+
+        def load_z(k):
+            zt = zpool.tile([P, 2, P, 16], BF16, name="zb%d" % k, tag="zb")
+            nc.sync.dma_start(
+                out=zt[:].rearrange("p j q v -> p (j q v)"),
+                in_=z_view[k].partition_broadcast(P),
+            )
+            zb[k] = zt
+
+        def load_x(c):
+            nc.sync.dma_start(out=xn[c][:], in_=x_view[:, 4 * c : 4 * c + 4, :])
+
+        load_x(0)
+        load_z(0)
+        nc.sync.dma_start(out=wraw0[:], in_=W0)
+        load_x(1)
+        load_z(1)
+        nc.sync.dma_start(out=wraw1[0:64, :, :], in_=W1)
+        nc.sync.dma_start(out=wraw2[0:32, :, :], in_=W2)
+        load_x(2)
+        load_x(3)
+        load_z(2)
+
+        nc.vector.tensor_copy(
+            out=sel0[:].rearrange("k (G s a) -> k G s a", G=4, s=8, a=4),
+            in_=ident[:].rearrange("k (G a s) -> k G s a", G=4, a=4, s=8),
+        )
+        for h in range(2):
+            nc.vector.tensor_copy(
+                out=sel1[:, 64 * h : 64 * h + 64].rearrange("k (G s a) -> k G s a", G=2, s=8, a=4),
+                in_=ident[:, 0:64].rearrange("k (G a s) -> k G s a", G=2, a=4, s=8),
+            )
+        for r in range(4):
+            nc.vector.tensor_copy(
+                out=sel2[:, 32 * r : 32 * r + 32].rearrange("k (s a) -> k s a", s=8, a=4),
+                in_=ident[:, 0:32].rearrange("k (a s) -> k s a", a=4, s=8),
+            )
+
+        xtd = {}
+        codes = {}
+
+        def stage_a(j):
+            src = xn[j // 4]
+            jj = j % 4
+            dst = xa[j % 4]
+            nc.scalar.copy(
+                out=dst[:, 0:128].rearrange("p (G s a) -> p G s a", G=4, s=8, a=4),
+                in_=src[:, jj, 0:128].rearrange("p (G a s) -> p G s a", G=4, a=4, s=8),
+            )
+            d1 = dst[:, 128:320].rearrange("p (i G s a) -> p i G s a", i=3, G=2, s=8, a=4)
+            r1 = src[:, jj, 128:320].rearrange("p (G a s i) -> p i G s a", G=2, a=4, s=8, i=3)
+            for G in range(2):
+                nc.scalar.copy(out=d1[:, :, G, :, :], in_=r1[:, :, G, :, :])
+            nc.scalar.copy(
+                out=dst[:, 320:480].rearrange("p (i s a) -> p i s a", i=5, s=8, a=4),
+                in_=src[:, jj, 320:480].rearrange("p (a s i) -> p i s a", a=4, s=8, i=5),
+            )
+            xt = ps_t.tile([P, 1024], BF16, name="xt%d" % j, tag="tp")
+            for T in range(4):
+                nc.tensor.transpose(xt[:, T * P : (T + 1) * P], dst[:, T * P : (T + 1) * P], ident[:])
+            xd = xtpool.tile([P, 512, 2], BF16, name="xtd%d" % j, tag="xtd")
+            nc.scalar.copy(out=xd[:], in_=xt[:, 0:512].unsqueeze(2).to_broadcast([P, 512, 2]))
+            xtd[j] = xd
+
+        def stage_b(j):
+            zt = zb[j // 2]
+            xd = xtd[j]
+            cj = cpool.tile([P, 4, 512], U32, name="cj%d" % j, tag="cj", align_bytes=64)
+            sj = cpool.tile([P, 4, 512], U8, name="sj%d" % j, tag="sj", align_bytes=64)
+            in0 = xd[:].rearrange("p (T q) b -> p T q b", T=4).unsqueeze(3).to_broadcast([P, 4, P, 2, 2])
+            pts = []
+            for h in range(2):
+                pt = ppool.tile([P, 4096], BF16, name="pt%d_%d" % (j, h), tag="pt", align_bytes=64)
+                pts.append(pt)
+                for gg in range(2):
+                    g = 2 * h + gg
+                    in1 = (
+                        zt[:, j % 2, :, 4 * g : 4 * g + 4]
+                        .rearrange("p q (a b) -> p q a b", a=2)
+                        .unsqueeze(1)
+                        .to_broadcast([P, 4, P, 2, 2])
+                    )
+                    nc.vector.tensor_tensor(
+                        out=pt[:, gg * 2048 : (gg + 1) * 2048].rearrange(
+                            "p (T q a b) -> p T q a b", T=4, q=P, a=2, b=2
+                        ),
+                        in0=in0,
+                        in1=in1,
+                        op=MULT,
+                    )
+            for h in range(2):
+                nc.vector.quantize_mx(
+                    out=cj[:, 2 * h : 2 * h + 2, :].rearrange("p g c -> p (g c)").bitcast(FP8X4),
+                    scales=sj[:, 2 * h : 2 * h + 2, :].rearrange("p g c -> p (g c)"),
+                    in_=pts[h][:],
+                )
+            codes[j] = (cj, sj)
+
+        def mx_group(acc, cj, sj, T, rhs, rhs_scale):
+            for g in range(4):
+                nc.tensor.matmul_mx(
+                    out=acc,
+                    lhsT=cj[:, g, T * P : (T + 1) * P].bitcast(FP8X4),
+                    lhsT_scale=sj[:, g, T * P : (T + 1) * P],
+                    rhs=rhs(g).bitcast(FP8X4),
+                    rhs_scale=rhs_scale(g),
+                    start=(g == 0),
+                    stop=(g == 3),
+                )
+
+        def stage_c(j):
+            cj, sj = codes[j]
+            ost = opool.tile([P, 4, FEAT], F32, name="ost%d" % j, tag="ost")
+            o0 = ps_o.tile([P, 512], F32, name="o0_%d" % j, tag="o0")
+            mx_group(o0[:], cj, sj, 0, lambda g: w0c[:, g, :], lambda g: w0s[:, g, :])
+            nc.scalar.activation(
+                out=ost[:, :, 0:128], in_=o0[:].rearrange("p (c w) -> p c w", c=4), func=COPY, scale=ALPHA0
+            )
+            for cp in range(2):
+                o1 = ps_o.tile([P, 512], F32, name="o1_%d_%d" % (j, cp), tag="o1_%d" % cp)
+                mx_group(
+                    o1[:, 0:256], cj, sj, 1,
+                    lambda g: m1[:, 2 * g + cp, 0:256], lambda g: sm1[:, 2 * g + cp, 0:256],
+                )
+                mx_group(
+                    o1[:, 256:384], cj, sj, 2,
+                    lambda g: m1[:, 2 * g + cp, 0:128], lambda g: sm1[:, 2 * g + cp, 0:128],
+                )
+                nc.scalar.activation(
+                    out=ost[:, 2 * cp : 2 * cp + 2, 128:320].rearrange("p c (w i) -> p c w i", i=3),
+                    in_=o1[:, 0:384].rearrange("p (i c w) -> p c w i", i=3, c=2),
+                    func=COPY,
+                    scale=ALPHA1,
+                )
+            for cp in range(2):
+                o2 = ps_o.tile([P, 512], F32, name="o2_%d_%d" % (j, cp), tag="o2_%d" % cp)
+                mx_group(
+                    o2[:, 0:128], cj, sj, 2,
+                    lambda g: m2[:, 2 * g + cp, 128:256], lambda g: sm2[:, 2 * g + cp, 128:256],
+                )
+                mx_group(
+                    o2[:, 128:384], cj, sj, 3,
+                    lambda g: m2[:, 2 * g + cp, 0:256], lambda g: sm2[:, 2 * g + cp, 0:256],
+                )
+                nc.scalar.activation(
+                    out=ost[:, 2 * cp : 2 * cp + 2, 320:480].rearrange("p c (w i) -> p c w i", i=5),
+                    in_=o2[:, 0:320].rearrange("p (i c w) -> p c w i", i=5, c=2),
+                    func=COPY,
+                    scale=ALPHA2,
+                )
+            nc.scalar.dma_start(out=out_view[j], in_=ost[:].rearrange("p c f -> p (c f)"))
+
+        def select_rows(ws, col, width, sel, rhs):
+            nc.tensor.matmul(out=ws[:, col : col + width], lhsT=sel[:], rhs=rhs, start=True, stop=True)
+
+        def prep_w0():
+            for h in range(2):
+                wg = wgpool.tile([P, 4096], BF16, name="wg0_%d" % h, tag="wg", align_bytes=64)
+                for gg in range(2):
+                    g = 2 * h + gg
+                    for wh in range(2):
+                        ws = ps_t.tile([P, 1024], BF16, name="ws0_%d_%d" % (g, wh), tag="tp")
+                        for t in range(4):
+                            select_rows(ws, t * 256, 256, sel0, wraw0[:, 4 * g + t, wh * 256 : (wh + 1) * 256])
+                        off = gg * 2048 + wh * 1024
+                        nc.scalar.copy(
+                            out=wg[:, off : off + 1024].rearrange("p (w t) -> p w t", t=4),
+                            in_=ws[:].rearrange("p (t w) -> p w t", t=4),
+                        )
+                nc.vector.quantize_mx(
+                    out=w0c[:, 2 * h : 2 * h + 2, :].rearrange("p g c -> p (g c)").bitcast(FP8X4),
+                    scales=w0s[:, 2 * h : 2 * h + 2, :].rearrange("p g c -> p (g c)"),
+                    in_=wg[:],
+                )
+
+        def prep_w1():
+            wg = wgpool.tile([P, 4096], BF16, name="wg1", tag="wg", align_bytes=64)
+            for g in range(4):
+                ws = ps_t.tile([P, 1024], BF16, name="ws1_%d" % g, tag="tp")
+                for t in range(4):
+                    select_rows(ws, t * 256, 256, sel1, wraw1[:, 4 * g + t, :])
+                nc.scalar.copy(
+                    out=wg[:, g * 1024 : (g + 1) * 1024].rearrange("p (w t) -> p w t", t=4),
+                    in_=ws[:].rearrange("p (t w) -> p w t", t=4),
+                )
+            nc.vector.quantize_mx(
+                out=c1[:].rearrange("p a c -> p (a c)").bitcast(FP8X4),
+                scales=s1[:].rearrange("p a c -> p (a c)"),
+                in_=wg[:],
+            )
+            for h in range(2):
+                rows = slice(64 * h, 64 * h + 64)
+                nc.vector.tensor_copy(
+                    out=m1[rows, :, 128 * h : 128 * h + 128].bitcast(I32), in_=c1[rows, :, :].bitcast(I32)
+                )
+                nc.vector.tensor_copy(
+                    out=sm1[:].bitcast(I32)[:, :, 32 * h : 32 * h + 32], in_=s1[:].bitcast(I32)
+                )
+
+        def prep_w2():
+            wg = wgpool.tile([P, 4096], BF16, name="wg2", tag="wg", align_bytes=64)
+            for gp in range(2):
+                ws = ps_t.tile([P, 1024], BF16, name="ws2_%d" % gp, tag="tp")
+                for b in range(2):
+                    for t in range(4):
+                        select_rows(ws, (b * 4 + t) * 128, 128, sel2, wraw2[:, 4 * (2 * gp + b) + t, :])
+                nc.scalar.copy(
+                    out=wg[:, gp * 1024 : (gp + 1) * 1024].rearrange("p (b w t) -> p b w t", b=2, t=4),
+                    in_=ws[:].rearrange("p (b t w) -> p b w t", b=2, t=4),
+                )
+            nc.vector.quantize_mx(
+                out=c2[:].rearrange("p a c -> p (a c)").bitcast(FP8X4),
+                scales=s2[:].rearrange("p a c -> p (a c)"),
+                in_=wg[:, 0:2048],
+            )
+            for r in range(4):
+                rows = slice(32 * r, 32 * r + 32)
+                nc.vector.tensor_copy(
+                    out=m2[rows, :, 64 * r : 64 * r + 64].bitcast(I32), in_=c2[rows, :, :].bitcast(I32)
+                )
+                nc.vector.tensor_copy(
+                    out=sm2[:].bitcast(I32)[:, :, 16 * r : 16 * r + 16], in_=s2[:].bitcast(I32)
+                )
+
+        stage_a(0)
+        stage_a(1)
+        stage_b(0)
+        prep_w0()
+        stage_a(2)
+        stage_b(1)
+        prep_w1()
+        prep_w2()
+        for j in range(NJ):
+            if j + 3 < NJ:
+                stage_a(j + 3)
+            if j + 2 < NJ:
+                if (j + 2) % 2 == 0 and (j + 2) // 2 + 2 < NJ // 2:
+                    load_z((j + 2) // 2 + 2)
+                stage_b(j + 2)
+            stage_c(j)

@@ -22,6 +22,7 @@ FLOPS = 2 * NODES * (1 * 2048 * 512 + 3 * 1024 * 256 + 5 * 512 * 128)
 ALPHA0 = 1.0 / math.sqrt(2048.0)
 ALPHA1 = 1.0 / math.sqrt(1024.0)
 ALPHA2 = 1.0 / math.sqrt(512.0)
+DIAG_TILES = (3, 5, 7, 9, 10, 11, 12, 13, 14, 15)
 
 
 def tile_tensorproductselfinteraction_kernel(tc, node_embeddings, Z_embeddings, W0, W1, W2, out):
@@ -36,14 +37,17 @@ def tile_tensorproductselfinteraction_kernel(tc, node_embeddings, Z_embeddings, 
         xtpool = ctx.enter_context(tc.tile_pool(name="xtpool", bufs=3))
         ppool = ctx.enter_context(tc.tile_pool(name="ppool", bufs=3))
         wgpool = ctx.enter_context(tc.tile_pool(name="wgpool", bufs=2))
-        cpool = ctx.enter_context(tc.tile_pool(name="cpool", bufs=4))
-        opool = ctx.enter_context(tc.tile_pool(name="opool", bufs=3))
+        cpool = ctx.enter_context(tc.tile_pool(name="cpool", bufs=6))
+        opool = ctx.enter_context(tc.tile_pool(name="opool", bufs=2))
+        dpool = ctx.enter_context(tc.tile_pool(name="dpool", bufs=3))
+        dzpool = ctx.enter_context(tc.tile_pool(name="dzpool", bufs=2))
         ps_t = ctx.enter_context(tc.psum_pool(name="ps_t", bufs=3))
         ps_o = ctx.enter_context(tc.psum_pool(name="ps_o", bufs=1))
 
         ident = const.tile([P, P], BF16, name="ident")
         make_identity(nc, ident[:])
-        sel0 = const.tile([P, P], BF16, name="sel0")
+        irep = const.tile([P, P, 4], BF16, name="irep")
+        znat = const.tile([P, NJ, 16], BF16, name="znat")
         sel1 = const.tile([P, P], BF16, name="sel1")
         sel2 = const.tile([P, P], BF16, name="sel2")
 
@@ -64,12 +68,10 @@ def tile_tensorproductselfinteraction_kernel(tc, node_embeddings, Z_embeddings, 
         xn = [const.tile([P, 4, FEAT], BF16, name="xn%d" % c) for c in range(4)]
         xa = [const.tile([P, 512], BF16, name="xa%d" % k) for k in range(4)]
 
-        nc.vector.memset(m1[:].bitcast(I32), 0)
-        nc.vector.memset(m2[:].bitcast(I32), 0)
+        nc.gpsimd.memset(m1[:].bitcast(F32), 0.0)
+        nc.gpsimd.memset(m2[:].bitcast(F32), 0.0)
         nc.vector.memset(s1[:].bitcast(I32), 0)
         nc.vector.memset(s2[:].bitcast(I32), 0)
-        nc.vector.memset(wraw1[64:128, :, :].bitcast(I32), 0)
-        nc.vector.memset(wraw2[:].bitcast(I32), 0)
         for k in range(4):
             nc.vector.memset(xa[k][:, FEAT:512].bitcast(I32), 0)
 
@@ -86,21 +88,33 @@ def tile_tensorproductselfinteraction_kernel(tc, node_embeddings, Z_embeddings, 
         def load_x(c):
             nc.sync.dma_start(out=xn[c][:], in_=x_view[:, 4 * c : 4 * c + 4, :])
 
-        load_x(0)
-        load_z(0)
-        nc.sync.dma_start(out=wraw0[:], in_=W0)
-        load_x(1)
+        nc.sync.dma_start(out=xn[0][:, 0:1, :], in_=x_view[:, 0:1, :])
+        z0 = zpool.tile([P, 2, P, 16], BF16, name="zb0", tag="zb")
+        zb[0] = z0
+        for jj in range(2):
+            nc.sync.dma_start(
+                out=z0[:, jj, :, :].rearrange("p q v -> p (q v)"),
+                in_=z_view[0][jj * 2048 : (jj + 1) * 2048].partition_broadcast(P),
+            )
+            if jj == 0:
+                nc.sync.dma_start(out=xn[0][:, 1:4, :], in_=x_view[:, 1:4, :])
+        for cc in range(4):
+            for e in range(2):
+                nc.sync.dma_start(
+                    out=wraw0[32 * cc + e : 32 * cc + 32 : 2, :, :], in_=W0[2 * cc + e : P : 8, :, :]
+                )
+        nc.sync.dma_start(out=znat[:], in_=Z_embeddings.rearrange("(j q) v -> q j v", q=P))
+        for h in range(2):
+            nc.sync.dma_start(out=wraw1[64 * h : 64 * h + 64, :, :], in_=W1)
+        for r in range(4):
+            nc.sync.dma_start(out=wraw2[32 * r : 32 * r + 32, :, :], in_=W2)
         load_z(1)
-        nc.sync.dma_start(out=wraw1[0:64, :, :], in_=W1)
-        nc.sync.dma_start(out=wraw2[0:32, :, :], in_=W2)
+        load_x(1)
+        load_z(2)
         load_x(2)
         load_x(3)
-        load_z(2)
 
-        nc.vector.tensor_copy(
-            out=sel0[:].rearrange("k (G s a) -> k G s a", G=4, s=8, a=4),
-            in_=ident[:].rearrange("k (G a s) -> k G s a", G=4, a=4, s=8),
-        )
+        nc.vector.tensor_copy(out=irep[:], in_=ident[:].unsqueeze(2).to_broadcast([P, P, 4]))
         for h in range(2):
             nc.vector.tensor_copy(
                 out=sel1[:, 64 * h : 64 * h + 64].rearrange("k (G s a) -> k G s a", G=2, s=8, a=4),
@@ -114,14 +128,15 @@ def tile_tensorproductselfinteraction_kernel(tc, node_embeddings, Z_embeddings, 
 
         xtd = {}
         codes = {}
+        diag = {}
 
         def stage_a(j):
             src = xn[j // 4]
             jj = j % 4
             dst = xa[j % 4]
             nc.scalar.copy(
-                out=dst[:, 0:128].rearrange("p (G s a) -> p G s a", G=4, s=8, a=4),
-                in_=src[:, jj, 0:128].rearrange("p (G a s) -> p G s a", G=4, a=4, s=8),
+                out=dst[:, 0:128].rearrange("p (c A e) -> p c A e", c=4, A=16, e=2),
+                in_=src[:, jj, 0:128].rearrange("p (A c e) -> p c A e", A=16, c=4, e=2),
             )
             d1 = dst[:, 128:320].rearrange("p (i G s a) -> p i G s a", i=3, G=2, s=8, a=4)
             r1 = src[:, jj, 128:320].rearrange("p (G a s i) -> p i G s a", G=2, a=4, s=8, i=3)
@@ -137,6 +152,28 @@ def tile_tensorproductselfinteraction_kernel(tc, node_embeddings, Z_embeddings, 
             xd = xtpool.tile([P, 512, 2], BF16, name="xtd%d" % j, tag="xtd")
             nc.scalar.copy(out=xd[:], in_=xt[:, 0:512].unsqueeze(2).to_broadcast([P, 512, 2]))
             xtd[j] = xd
+            if j in DIAG_TILES:
+                dz = dzpool.tile([P, 512], BF16, name="dz%d" % j, tag="dz")
+                nc.vector.tensor_tensor(
+                    out=dz[:].rearrange("p (q t) -> p q t", t=4),
+                    in0=irep[:],
+                    in1=znat[:, j, 12:16].unsqueeze(1).to_broadcast([P, P, 4]),
+                    op=MULT,
+                )
+                dg = dpool.tile([P, 2048], BF16, name="dg%d" % j, tag="dg", align_bytes=64)
+                for half in range(2):
+                    pd = ps_t.tile([P, 1024], BF16, name="pd%d_%d" % (j, half), tag="tp")
+                    for tt in range(2):
+                        T = 2 * half + tt
+                        nc.tensor.matmul(
+                            out=pd[:, tt * 512 : (tt + 1) * 512],
+                            lhsT=dst[:, T * P : (T + 1) * P],
+                            rhs=dz[:],
+                            start=True,
+                            stop=True,
+                        )
+                    nc.scalar.copy(out=dg[:, half * 1024 : (half + 1) * 1024], in_=pd[:])
+                diag[j] = dg
 
         def stage_b(j):
             zt = zb[j // 2]
@@ -150,6 +187,8 @@ def tile_tensorproductselfinteraction_kernel(tc, node_embeddings, Z_embeddings, 
                 pts.append(pt)
                 for gg in range(2):
                     g = 2 * h + gg
+                    if g == 3 and j in DIAG_TILES:
+                        continue
                     in1 = (
                         zt[:, j % 2, :, 4 * g : 4 * g + 4]
                         .rearrange("p q (a b) -> p q a b", a=2)
@@ -164,11 +203,20 @@ def tile_tensorproductselfinteraction_kernel(tc, node_embeddings, Z_embeddings, 
                         in1=in1,
                         op=MULT,
                     )
-            for h in range(2):
+            if j in DIAG_TILES:
+                nc.vector.quantize_mx(out=cj[:, 3, :].bitcast(FP8X4), scales=sj[:, 3, :], in_=diag[j][:])
+            nc.vector.quantize_mx(
+                out=cj[:, 0:2, :].rearrange("p g c -> p (g c)").bitcast(FP8X4),
+                scales=sj[:, 0:2, :].rearrange("p g c -> p (g c)"),
+                in_=pts[0][:],
+            )
+            if j in DIAG_TILES:
+                nc.vector.quantize_mx(out=cj[:, 2, :].bitcast(FP8X4), scales=sj[:, 2, :], in_=pts[1][:, 0:2048])
+            else:
                 nc.vector.quantize_mx(
-                    out=cj[:, 2 * h : 2 * h + 2, :].rearrange("p g c -> p (g c)").bitcast(FP8X4),
-                    scales=sj[:, 2 * h : 2 * h + 2, :].rearrange("p g c -> p (g c)"),
-                    in_=pts[h][:],
+                    out=cj[:, 2:4, :].rearrange("p g c -> p (g c)").bitcast(FP8X4),
+                    scales=sj[:, 2:4, :].rearrange("p g c -> p (g c)"),
+                    in_=pts[1][:],
                 )
             codes[j] = (cj, sj)
 
@@ -230,40 +278,31 @@ def tile_tensorproductselfinteraction_kernel(tc, node_embeddings, Z_embeddings, 
             nc.tensor.matmul(out=ws[:, col : col + width], lhsT=sel[:], rhs=rhs, start=True, stop=True)
 
         def prep_w0():
-            for h in range(2):
-                wg = wgpool.tile([P, 4096], BF16, name="wg0_%d" % h, tag="wg", align_bytes=64)
-                for gg in range(2):
-                    g = 2 * h + gg
-                    for wh in range(2):
-                        ws = ps_t.tile([P, 1024], BF16, name="ws0_%d_%d" % (g, wh), tag="tp")
-                        for t in range(4):
-                            select_rows(ws, t * 256, 256, sel0, wraw0[:, 4 * g + t, wh * 256 : (wh + 1) * 256])
-                        off = gg * 2048 + wh * 1024
-                        nc.scalar.copy(
-                            out=wg[:, off : off + 1024].rearrange("p (w t) -> p w t", t=4),
-                            in_=ws[:].rearrange("p (t w) -> p w t", t=4),
-                        )
-                nc.vector.quantize_mx(
-                    out=w0c[:, 2 * h : 2 * h + 2, :].rearrange("p g c -> p (g c)").bitcast(FP8X4),
-                    scales=w0s[:, 2 * h : 2 * h + 2, :].rearrange("p g c -> p (g c)"),
-                    in_=wg[:],
+            for g in range(4):
+                wg = wgpool.tile([P, 2048], BF16, name="wg0_%d" % g, tag="wg", align_bytes=64)
+                nc.scalar.copy(
+                    out=wg[:].rearrange("p (c i t) -> p c t i", i=4, t=4),
+                    in_=wraw0[:, 4 * g : 4 * g + 4, :].rearrange("p t (c i) -> p c t i", i=4),
                 )
+                nc.vector.quantize_mx(out=w0c[:, g, :].bitcast(FP8X4), scales=w0s[:, g, :], in_=wg[:])
 
         def prep_w1():
-            wg = wgpool.tile([P, 4096], BF16, name="wg1", tag="wg", align_bytes=64)
-            for g in range(4):
-                ws = ps_t.tile([P, 1024], BF16, name="ws1_%d" % g, tag="tp")
-                for t in range(4):
-                    select_rows(ws, t * 256, 256, sel1, wraw1[:, 4 * g + t, :])
-                nc.scalar.copy(
-                    out=wg[:, g * 1024 : (g + 1) * 1024].rearrange("p (w t) -> p w t", t=4),
-                    in_=ws[:].rearrange("p (t w) -> p w t", t=4),
+            for gp in range(2):
+                wg = wgpool.tile([P, 2048], BF16, name="wg1_%d" % gp, tag="wg", align_bytes=64)
+                for gg in range(2):
+                    g = 2 * gp + gg
+                    ws = ps_t.tile([P, 1024], BF16, name="ws1_%d" % g, tag="tp")
+                    for t in range(4):
+                        select_rows(ws, t * 256, 256, sel1, wraw1[:, 4 * g + t, :])
+                    nc.scalar.copy(
+                        out=wg[:, gg * 1024 : (gg + 1) * 1024].rearrange("p (w t) -> p w t", t=4),
+                        in_=ws[:].rearrange("p (t w) -> p w t", t=4),
+                    )
+                nc.vector.quantize_mx(
+                    out=c1[:, 4 * gp : 4 * gp + 4, :].rearrange("p a c -> p (a c)").bitcast(FP8X4),
+                    scales=s1[:, 4 * gp : 4 * gp + 4, :].rearrange("p a c -> p (a c)"),
+                    in_=wg[:],
                 )
-            nc.vector.quantize_mx(
-                out=c1[:].rearrange("p a c -> p (a c)").bitcast(FP8X4),
-                scales=s1[:].rearrange("p a c -> p (a c)"),
-                in_=wg[:],
-            )
             for h in range(2):
                 rows = slice(64 * h, 64 * h + 64)
                 nc.vector.tensor_copy(
@@ -274,7 +313,7 @@ def tile_tensorproductselfinteraction_kernel(tc, node_embeddings, Z_embeddings, 
                 )
 
         def prep_w2():
-            wg = wgpool.tile([P, 4096], BF16, name="wg2", tag="wg", align_bytes=64)
+            wg = wgpool.tile([P, 2048], BF16, name="wg2", tag="wg", align_bytes=64)
             for gp in range(2):
                 ws = ps_t.tile([P, 1024], BF16, name="ws2_%d" % gp, tag="tp")
                 for b in range(2):
@@ -287,7 +326,7 @@ def tile_tensorproductselfinteraction_kernel(tc, node_embeddings, Z_embeddings, 
             nc.vector.quantize_mx(
                 out=c2[:].rearrange("p a c -> p (a c)").bitcast(FP8X4),
                 scales=s2[:].rearrange("p a c -> p (a c)"),
-                in_=wg[:, 0:2048],
+                in_=wg[:],
             )
             for r in range(4):
                 rows = slice(32 * r, 32 * r + 32)

@@ -22,7 +22,7 @@ FLOPS = 2 * NODES * (1 * 2048 * 512 + 3 * 1024 * 256 + 5 * 512 * 128)
 ALPHA0 = 1.0 / math.sqrt(2048.0)
 ALPHA1 = 1.0 / math.sqrt(1024.0)
 ALPHA2 = 1.0 / math.sqrt(512.0)
-DIAG_TILES = (3, 5, 7, 9, 10, 11, 12, 13, 14, 15)
+POOL_PASSES = (2, 0, 1)
 
 
 def tile_tensorproductselfinteraction_kernel(tc, node_embeddings, Z_embeddings, W0, W1, W2, out):
@@ -34,20 +34,16 @@ def tile_tensorproductselfinteraction_kernel(tc, node_embeddings, Z_embeddings, 
     with ExitStack() as ctx:
         const = ctx.enter_context(tc.tile_pool(name="const", bufs=1))
         zpool = ctx.enter_context(tc.tile_pool(name="zpool", bufs=3))
-        xtpool = ctx.enter_context(tc.tile_pool(name="xtpool", bufs=3))
-        ppool = ctx.enter_context(tc.tile_pool(name="ppool", bufs=3))
+        xspool = ctx.enter_context(tc.tile_pool(name="xspool", bufs=3))
         wgpool = ctx.enter_context(tc.tile_pool(name="wgpool", bufs=2))
-        cpool = ctx.enter_context(tc.tile_pool(name="cpool", bufs=6))
-        opool = ctx.enter_context(tc.tile_pool(name="opool", bufs=2))
-        dpool = ctx.enter_context(tc.tile_pool(name="dpool", bufs=3))
-        dzpool = ctx.enter_context(tc.tile_pool(name="dzpool", bufs=2))
+        cpool = ctx.enter_context(tc.tile_pool(name="cpool", bufs=5))
+        opool = ctx.enter_context(tc.tile_pool(name="opool", bufs=3))
         ps_t = ctx.enter_context(tc.psum_pool(name="ps_t", bufs=3))
         ps_o = ctx.enter_context(tc.psum_pool(name="ps_o", bufs=1))
 
         ident = const.tile([P, P], BF16, name="ident")
         make_identity(nc, ident[:])
-        irep = const.tile([P, P, 4], BF16, name="irep")
-        znat = const.tile([P, NJ, 16], BF16, name="znat")
+        idup = const.tile([P, P, 2], BF16, name="idup")
         sel1 = const.tile([P, P], BF16, name="sel1")
         sel2 = const.tile([P, P], BF16, name="sel2")
 
@@ -67,6 +63,7 @@ def tile_tensorproductselfinteraction_kernel(tc, node_embeddings, Z_embeddings, 
         wraw2 = const.tile([P, 16, 128], BF16, name="wraw2")
         xn = [const.tile([P, 4, FEAT], BF16, name="xn%d" % c) for c in range(4)]
         xa = [const.tile([P, 512], BF16, name="xa%d" % k) for k in range(4)]
+        prod = const.tile([P, 4, 2048], BF16, name="prod", align_bytes=64)
 
         nc.gpsimd.memset(m1[:].bitcast(F32), 0.0)
         nc.gpsimd.memset(m2[:].bitcast(F32), 0.0)
@@ -103,7 +100,6 @@ def tile_tensorproductselfinteraction_kernel(tc, node_embeddings, Z_embeddings, 
                 nc.sync.dma_start(
                     out=wraw0[32 * cc + e : 32 * cc + 32 : 2, :, :], in_=W0[2 * cc + e : P : 8, :, :]
                 )
-        nc.sync.dma_start(out=znat[:], in_=Z_embeddings.rearrange("(j q) v -> q j v", q=P))
         for h in range(2):
             nc.sync.dma_start(out=wraw1[64 * h : 64 * h + 64, :, :], in_=W1)
         for r in range(4):
@@ -114,7 +110,7 @@ def tile_tensorproductselfinteraction_kernel(tc, node_embeddings, Z_embeddings, 
         load_x(2)
         load_x(3)
 
-        nc.vector.tensor_copy(out=irep[:], in_=ident[:].unsqueeze(2).to_broadcast([P, P, 4]))
+        nc.vector.tensor_copy(out=idup[:], in_=ident[:].unsqueeze(2).to_broadcast([P, P, 2]))
         for h in range(2):
             nc.vector.tensor_copy(
                 out=sel1[:, 64 * h : 64 * h + 64].rearrange("k (G s a) -> k G s a", G=2, s=8, a=4),
@@ -127,8 +123,8 @@ def tile_tensorproductselfinteraction_kernel(tc, node_embeddings, Z_embeddings, 
             )
 
         xtd = {}
+        xsb = {}
         codes = {}
-        diag = {}
 
         def stage_a(j):
             src = xn[j // 4]
@@ -148,75 +144,49 @@ def tile_tensorproductselfinteraction_kernel(tc, node_embeddings, Z_embeddings, 
             )
             xt = ps_t.tile([P, 1024], BF16, name="xt%d" % j, tag="tp")
             for T in range(4):
-                nc.tensor.transpose(xt[:, T * P : (T + 1) * P], dst[:, T * P : (T + 1) * P], ident[:])
-            xd = xtpool.tile([P, 512, 2], BF16, name="xtd%d" % j, tag="xtd")
-            nc.scalar.copy(out=xd[:], in_=xt[:, 0:512].unsqueeze(2).to_broadcast([P, 512, 2]))
-            xtd[j] = xd
-            if j in DIAG_TILES:
-                dz = dzpool.tile([P, 512], BF16, name="dz%d" % j, tag="dz")
-                nc.vector.tensor_tensor(
-                    out=dz[:].rearrange("p (q t) -> p q t", t=4),
-                    in0=irep[:],
-                    in1=znat[:, j, 12:16].unsqueeze(1).to_broadcast([P, P, 4]),
-                    op=MULT,
+                nc.tensor.matmul(
+                    out=xt[:, T * 256 : (T + 1) * 256],
+                    lhsT=dst[:, T * P : (T + 1) * P],
+                    rhs=idup[:].rearrange("p q b -> p (q b)"),
+                    start=True,
+                    stop=True,
                 )
-                dg = dpool.tile([P, 2048], BF16, name="dg%d" % j, tag="dg", align_bytes=64)
-                for half in range(2):
-                    pd = ps_t.tile([P, 1024], BF16, name="pd%d_%d" % (j, half), tag="tp")
-                    for tt in range(2):
-                        T = 2 * half + tt
-                        nc.tensor.matmul(
-                            out=pd[:, tt * 512 : (tt + 1) * 512],
-                            lhsT=dst[:, T * P : (T + 1) * P],
-                            rhs=dz[:],
-                            start=True,
-                            stop=True,
-                        )
-                    nc.scalar.copy(out=dg[:, half * 1024 : (half + 1) * 1024], in_=pd[:])
-                diag[j] = dg
+            xtd[j] = xt
+            xs = xspool.tile([P, P], BF16, name="xs%d" % j, tag="xs")
+            nc.scalar.copy(out=xs[:], in_=xt[:, 768:1024].rearrange("p (q b) -> p q b", b=2)[:, :, 0])
+            xsb[j] = xs
 
         def stage_b(j):
             zt = zb[j // 2]
             xd = xtd[j]
             cj = cpool.tile([P, 4, 512], U32, name="cj%d" % j, tag="cj", align_bytes=64)
             sj = cpool.tile([P, 4, 512], U8, name="sj%d" % j, tag="sj", align_bytes=64)
-            in0 = xd[:].rearrange("p (T q) b -> p T q b", T=4).unsqueeze(3).to_broadcast([P, 4, P, 2, 2])
-            pts = []
+            for g in POOL_PASSES:
+                nc.gpsimd.tensor_tensor(
+                    out=prod[:, g, 1536:2048].rearrange("p (q t) -> p q t", t=4),
+                    in0=xsb[j][:].unsqueeze(2).to_broadcast([P, P, 4]),
+                    in1=zt[:, j % 2, :, 4 * g : 4 * g + 4],
+                    op=MULT,
+                )
+            for g in range(4):
+                nt = 3 if g in POOL_PASSES else 4
+                nc.vector.tensor_tensor(
+                    out=prod[:, g, 0 : nt * 512].rearrange("p (T q a b) -> p T q a b", T=nt, q=P, a=2, b=2),
+                    in0=xd[:, 0 : nt * 256]
+                    .rearrange("p (T q b) -> p T q b", T=nt, b=2)
+                    .unsqueeze(3)
+                    .to_broadcast([P, nt, P, 2, 2]),
+                    in1=zt[:, j % 2, :, 4 * g : 4 * g + 4]
+                    .rearrange("p q (a b) -> p q a b", a=2)
+                    .unsqueeze(1)
+                    .to_broadcast([P, nt, P, 2, 2]),
+                    op=MULT,
+                )
             for h in range(2):
-                pt = ppool.tile([P, 4096], BF16, name="pt%d_%d" % (j, h), tag="pt", align_bytes=64)
-                pts.append(pt)
-                for gg in range(2):
-                    g = 2 * h + gg
-                    if g == 3 and j in DIAG_TILES:
-                        continue
-                    in1 = (
-                        zt[:, j % 2, :, 4 * g : 4 * g + 4]
-                        .rearrange("p q (a b) -> p q a b", a=2)
-                        .unsqueeze(1)
-                        .to_broadcast([P, 4, P, 2, 2])
-                    )
-                    nc.vector.tensor_tensor(
-                        out=pt[:, gg * 2048 : (gg + 1) * 2048].rearrange(
-                            "p (T q a b) -> p T q a b", T=4, q=P, a=2, b=2
-                        ),
-                        in0=in0,
-                        in1=in1,
-                        op=MULT,
-                    )
-            if j in DIAG_TILES:
-                nc.vector.quantize_mx(out=cj[:, 3, :].bitcast(FP8X4), scales=sj[:, 3, :], in_=diag[j][:])
-            nc.vector.quantize_mx(
-                out=cj[:, 0:2, :].rearrange("p g c -> p (g c)").bitcast(FP8X4),
-                scales=sj[:, 0:2, :].rearrange("p g c -> p (g c)"),
-                in_=pts[0][:],
-            )
-            if j in DIAG_TILES:
-                nc.vector.quantize_mx(out=cj[:, 2, :].bitcast(FP8X4), scales=sj[:, 2, :], in_=pts[1][:, 0:2048])
-            else:
                 nc.vector.quantize_mx(
-                    out=cj[:, 2:4, :].rearrange("p g c -> p (g c)").bitcast(FP8X4),
-                    scales=sj[:, 2:4, :].rearrange("p g c -> p (g c)"),
-                    in_=pts[1][:],
+                    out=cj[:, 2 * h : 2 * h + 2, :].rearrange("p g c -> p (g c)").bitcast(FP8X4),
+                    scales=sj[:, 2 * h : 2 * h + 2, :].rearrange("p g c -> p (g c)"),
+                    in_=prod[:, 2 * h : 2 * h + 2, :].rearrange("p g c -> p (g c)"),
                 )
             codes[j] = (cj, sj)
 
@@ -291,7 +261,7 @@ def tile_tensorproductselfinteraction_kernel(tc, node_embeddings, Z_embeddings, 
                 wg = wgpool.tile([P, 2048], BF16, name="wg1_%d" % gp, tag="wg", align_bytes=64)
                 for gg in range(2):
                     g = 2 * gp + gg
-                    ws = ps_t.tile([P, 1024], BF16, name="ws1_%d" % g, tag="tp")
+                    ws = ps_o.tile([P, 1024], BF16, name="ws1_%d" % g, tag="o2_%d" % gg)
                     for t in range(4):
                         select_rows(ws, t * 256, 256, sel1, wraw1[:, 4 * g + t, :])
                     nc.scalar.copy(
@@ -315,7 +285,7 @@ def tile_tensorproductselfinteraction_kernel(tc, node_embeddings, Z_embeddings, 
         def prep_w2():
             wg = wgpool.tile([P, 2048], BF16, name="wg2", tag="wg", align_bytes=64)
             for gp in range(2):
-                ws = ps_t.tile([P, 1024], BF16, name="ws2_%d" % gp, tag="tp")
+                ws = ps_o.tile([P, 1024], BF16, name="ws2_%d" % gp, tag="o2_%d" % gp)
                 for b in range(2):
                     for t in range(4):
                         select_rows(ws, (b * 4 + t) * 128, 128, sel2, wraw2[:, 4 * (2 * gp + b) + t, :])

@@ -22,7 +22,6 @@ FLOPS = 2 * NODES * (1 * 2048 * 512 + 3 * 1024 * 256 + 5 * 512 * 128)
 ALPHA0 = 1.0 / math.sqrt(2048.0)
 ALPHA1 = 1.0 / math.sqrt(1024.0)
 ALPHA2 = 1.0 / math.sqrt(512.0)
-POOL_PASSES = (2, 0, 1)
 
 
 def tile_tensorproductselfinteraction_kernel(tc, node_embeddings, Z_embeddings, W0, W1, W2, out):
@@ -34,7 +33,7 @@ def tile_tensorproductselfinteraction_kernel(tc, node_embeddings, Z_embeddings, 
     with ExitStack() as ctx:
         const = ctx.enter_context(tc.tile_pool(name="const", bufs=1))
         zpool = ctx.enter_context(tc.tile_pool(name="zpool", bufs=3))
-        xspool = ctx.enter_context(tc.tile_pool(name="xspool", bufs=3))
+        ppool = ctx.enter_context(tc.tile_pool(name="ppool", bufs=3))
         wgpool = ctx.enter_context(tc.tile_pool(name="wgpool", bufs=2))
         cpool = ctx.enter_context(tc.tile_pool(name="cpool", bufs=5))
         opool = ctx.enter_context(tc.tile_pool(name="opool", bufs=3))
@@ -63,7 +62,6 @@ def tile_tensorproductselfinteraction_kernel(tc, node_embeddings, Z_embeddings, 
         wraw2 = const.tile([P, 16, 128], BF16, name="wraw2")
         xn = [const.tile([P, 4, FEAT], BF16, name="xn%d" % c) for c in range(4)]
         xa = [const.tile([P, 512], BF16, name="xa%d" % k) for k in range(4)]
-        prod = const.tile([P, 4, 2048], BF16, name="prod", align_bytes=64)
 
         nc.gpsimd.memset(m1[:].bitcast(F32), 0.0)
         nc.gpsimd.memset(m2[:].bitcast(F32), 0.0)
@@ -123,7 +121,6 @@ def tile_tensorproductselfinteraction_kernel(tc, node_embeddings, Z_embeddings, 
             )
 
         xtd = {}
-        xsb = {}
         codes = {}
 
         def stage_a(j):
@@ -152,41 +149,38 @@ def tile_tensorproductselfinteraction_kernel(tc, node_embeddings, Z_embeddings, 
                     stop=True,
                 )
             xtd[j] = xt
-            xs = xspool.tile([P, P], BF16, name="xs%d" % j, tag="xs")
-            nc.scalar.copy(out=xs[:], in_=xt[:, 768:1024].rearrange("p (q b) -> p q b", b=2)[:, :, 0])
-            xsb[j] = xs
 
         def stage_b(j):
             zt = zb[j // 2]
             xd = xtd[j]
             cj = cpool.tile([P, 4, 512], U32, name="cj%d" % j, tag="cj", align_bytes=64)
             sj = cpool.tile([P, 4, 512], U8, name="sj%d" % j, tag="sj", align_bytes=64)
-            for g in POOL_PASSES:
-                nc.gpsimd.tensor_tensor(
-                    out=prod[:, g, 1536:2048].rearrange("p (q t) -> p q t", t=4),
-                    in0=xsb[j][:].unsqueeze(2).to_broadcast([P, P, 4]),
-                    in1=zt[:, j % 2, :, 4 * g : 4 * g + 4],
-                    op=MULT,
-                )
-            for g in range(4):
-                nt = 3 if g in POOL_PASSES else 4
-                nc.vector.tensor_tensor(
-                    out=prod[:, g, 0 : nt * 512].rearrange("p (T q a b) -> p T q a b", T=nt, q=P, a=2, b=2),
-                    in0=xd[:, 0 : nt * 256]
-                    .rearrange("p (T q b) -> p T q b", T=nt, b=2)
-                    .unsqueeze(3)
-                    .to_broadcast([P, nt, P, 2, 2]),
-                    in1=zt[:, j % 2, :, 4 * g : 4 * g + 4]
-                    .rearrange("p q (a b) -> p q a b", a=2)
-                    .unsqueeze(1)
-                    .to_broadcast([P, nt, P, 2, 2]),
-                    op=MULT,
-                )
+            in0 = xd[:].rearrange("p (T q b) -> p T q b", T=4, b=2).unsqueeze(3).to_broadcast([P, 4, P, 2, 2])
+            pts = []
+            for h in range(2):
+                pt = ppool.tile([P, 4096], BF16, name="pt%d_%d" % (j, h), tag="pt", align_bytes=64)
+                pts.append(pt)
+                for gg in range(2):
+                    g = 2 * h + gg
+                    in1 = (
+                        zt[:, j % 2, :, 4 * g : 4 * g + 4]
+                        .rearrange("p q (a b) -> p q a b", a=2)
+                        .unsqueeze(1)
+                        .to_broadcast([P, 4, P, 2, 2])
+                    )
+                    nc.vector.tensor_tensor(
+                        out=pt[:, gg * 2048 : (gg + 1) * 2048].rearrange(
+                            "p (T q a b) -> p T q a b", T=4, q=P, a=2, b=2
+                        ),
+                        in0=in0,
+                        in1=in1,
+                        op=MULT,
+                    )
             for h in range(2):
                 nc.vector.quantize_mx(
                     out=cj[:, 2 * h : 2 * h + 2, :].rearrange("p g c -> p (g c)").bitcast(FP8X4),
                     scales=sj[:, 2 * h : 2 * h + 2, :].rearrange("p g c -> p (g c)"),
-                    in_=prod[:, 2 * h : 2 * h + 2, :].rearrange("p g c -> p (g c)"),
+                    in_=pts[h][:],
                 )
             codes[j] = (cj, sj)
 

@@ -22,6 +22,7 @@ FLOPS = 2 * NODES * (1 * 2048 * 512 + 3 * 1024 * 256 + 5 * 512 * 128)
 ALPHA0 = 1.0 / math.sqrt(2048.0)
 ALPHA1 = 1.0 / math.sqrt(1024.0)
 ALPHA2 = 1.0 / math.sqrt(512.0)
+POOL_PASSES = (2, 0, 3)
 
 
 def tile_tensorproductselfinteraction_kernel(tc, node_embeddings, Z_embeddings, W0, W1, W2, out):
@@ -29,11 +30,12 @@ def tile_tensorproductselfinteraction_kernel(tc, node_embeddings, Z_embeddings, 
     x_view = node_embeddings.rearrange("(j q) f -> q j f", q=P)
     z_view = Z_embeddings.rearrange("(k n) v -> k (n v)", k=NJ // 2)
     out_view = out.rearrange("(j q c) f -> j q (c f)", q=P, c=4)
+    out_cols = out.rearrange("(j q c) f -> j q c f", q=P, c=4)
 
     with ExitStack() as ctx:
         const = ctx.enter_context(tc.tile_pool(name="const", bufs=1))
         zpool = ctx.enter_context(tc.tile_pool(name="zpool", bufs=3))
-        ppool = ctx.enter_context(tc.tile_pool(name="ppool", bufs=3))
+        xspool = ctx.enter_context(tc.tile_pool(name="xspool", bufs=3))
         wgpool = ctx.enter_context(tc.tile_pool(name="wgpool", bufs=2))
         cpool = ctx.enter_context(tc.tile_pool(name="cpool", bufs=5))
         opool = ctx.enter_context(tc.tile_pool(name="opool", bufs=3))
@@ -62,6 +64,7 @@ def tile_tensorproductselfinteraction_kernel(tc, node_embeddings, Z_embeddings, 
         wraw2 = const.tile([P, 16, 128], BF16, name="wraw2")
         xn = [const.tile([P, 4, FEAT], BF16, name="xn%d" % c) for c in range(4)]
         xa = [const.tile([P, 512], BF16, name="xa%d" % k) for k in range(4)]
+        prod = const.tile([P, 4, 2048], BF16, name="prod", align_bytes=64)
 
         nc.gpsimd.memset(m1[:].bitcast(F32), 0.0)
         nc.gpsimd.memset(m2[:].bitcast(F32), 0.0)
@@ -87,7 +90,7 @@ def tile_tensorproductselfinteraction_kernel(tc, node_embeddings, Z_embeddings, 
         z0 = zpool.tile([P, 2, P, 16], BF16, name="zb0", tag="zb")
         zb[0] = z0
         for jj in range(2):
-            nc.sync.dma_start(
+            nc.scalar.dma_start(
                 out=z0[:, jj, :, :].rearrange("p q v -> p (q v)"),
                 in_=z_view[0][jj * 2048 : (jj + 1) * 2048].partition_broadcast(P),
             )
@@ -121,6 +124,7 @@ def tile_tensorproductselfinteraction_kernel(tc, node_embeddings, Z_embeddings, 
             )
 
         xtd = {}
+        xsb = {}
         codes = {}
 
         def stage_a(j):
@@ -149,94 +153,138 @@ def tile_tensorproductselfinteraction_kernel(tc, node_embeddings, Z_embeddings, 
                     stop=True,
                 )
             xtd[j] = xt
+            xs = xspool.tile([P, P], BF16, name="xs%d" % j, tag="xs")
+            nc.scalar.copy(out=xs[:], in_=xt[:, 768:1024].rearrange("p (q b) -> p q b", b=2)[:, :, 0])
+            xsb[j] = xs
 
         def stage_b(j):
             zt = zb[j // 2]
             xd = xtd[j]
             cj = cpool.tile([P, 4, 512], U32, name="cj%d" % j, tag="cj", align_bytes=64)
             sj = cpool.tile([P, 4, 512], U8, name="sj%d" % j, tag="sj", align_bytes=64)
-            in0 = xd[:].rearrange("p (T q b) -> p T q b", T=4, b=2).unsqueeze(3).to_broadcast([P, 4, P, 2, 2])
-            pts = []
-            for h in range(2):
-                pt = ppool.tile([P, 4096], BF16, name="pt%d_%d" % (j, h), tag="pt", align_bytes=64)
-                pts.append(pt)
-                for gg in range(2):
-                    g = 2 * h + gg
-                    in1 = (
-                        zt[:, j % 2, :, 4 * g : 4 * g + 4]
-                        .rearrange("p q (a b) -> p q a b", a=2)
-                        .unsqueeze(1)
-                        .to_broadcast([P, 4, P, 2, 2])
-                    )
-                    nc.vector.tensor_tensor(
-                        out=pt[:, gg * 2048 : (gg + 1) * 2048].rearrange(
-                            "p (T q a b) -> p T q a b", T=4, q=P, a=2, b=2
-                        ),
-                        in0=in0,
-                        in1=in1,
-                        op=MULT,
-                    )
-            for h in range(2):
-                nc.vector.quantize_mx(
-                    out=cj[:, 2 * h : 2 * h + 2, :].rearrange("p g c -> p (g c)").bitcast(FP8X4),
-                    scales=sj[:, 2 * h : 2 * h + 2, :].rearrange("p g c -> p (g c)"),
-                    in_=pts[h][:],
+            for g in POOL_PASSES:
+                nc.gpsimd.tensor_tensor(
+                    out=prod[:, g, 1536:2048].rearrange("p (q t) -> p q t", t=4),
+                    in0=xsb[j][:].unsqueeze(2).to_broadcast([P, P, 4]),
+                    in1=zt[:, j % 2, :, 4 * g : 4 * g + 4],
+                    op=MULT,
                 )
+            for g in range(4):
+                nt = 3 if g in POOL_PASSES else 4
+                nc.vector.tensor_tensor(
+                    out=prod[:, g, 0 : nt * 512].rearrange("p (T q a b) -> p T q a b", T=nt, q=P, a=2, b=2),
+                    in0=xd[:, 0 : nt * 256]
+                    .rearrange("p (T q b) -> p T q b", T=nt, b=2)
+                    .unsqueeze(3)
+                    .to_broadcast([P, nt, P, 2, 2]),
+                    in1=zt[:, j % 2, :, 4 * g : 4 * g + 4]
+                    .rearrange("p q (a b) -> p q a b", a=2)
+                    .unsqueeze(1)
+                    .to_broadcast([P, nt, P, 2, 2]),
+                    op=MULT,
+                )
+            if j < NJ - 1:
+                for h in range(2):
+                    nc.vector.quantize_mx(
+                        out=cj[:, 2 * h : 2 * h + 2, :].rearrange("p g c -> p (g c)").bitcast(FP8X4),
+                        scales=sj[:, 2 * h : 2 * h + 2, :].rearrange("p g c -> p (g c)"),
+                        in_=prod[:, 2 * h : 2 * h + 2, :].rearrange("p g c -> p (g c)"),
+                    )
+            else:
+                for g in range(4):
+                    nc.vector.quantize_mx(out=cj[:, g, :].bitcast(FP8X4), scales=sj[:, g, :], in_=prod[:, g, :])
             codes[j] = (cj, sj)
 
-        def mx_group(acc, cj, sj, T, rhs, rhs_scale):
-            for g in range(4):
-                nc.tensor.matmul_mx(
-                    out=acc,
-                    lhsT=cj[:, g, T * P : (T + 1) * P].bitcast(FP8X4),
-                    lhsT_scale=sj[:, g, T * P : (T + 1) * P],
-                    rhs=rhs(g).bitcast(FP8X4),
-                    rhs_scale=rhs_scale(g),
-                    start=(g == 0),
-                    stop=(g == 3),
-                )
+        def mx_pass(acc, cj, sj, T, g, rhs, rhs_scale):
+            nc.tensor.matmul_mx(
+                out=acc,
+                lhsT=cj[:, g, T * P : (T + 1) * P].bitcast(FP8X4),
+                lhsT_scale=sj[:, g, T * P : (T + 1) * P],
+                rhs=rhs.bitcast(FP8X4),
+                rhs_scale=rhs_scale,
+                start=(g == 0),
+                stop=(g == 3),
+            )
 
         def stage_c(j):
             cj, sj = codes[j]
             ost = opool.tile([P, 4, FEAT], F32, name="ost%d" % j, tag="ost")
             o0 = ps_o.tile([P, 512], F32, name="o0_%d" % j, tag="o0")
-            mx_group(o0[:], cj, sj, 0, lambda g: w0c[:, g, :], lambda g: w0s[:, g, :])
-            nc.scalar.activation(
-                out=ost[:, :, 0:128], in_=o0[:].rearrange("p (c w) -> p c w", c=4), func=COPY, scale=ALPHA0
-            )
-            for cp in range(2):
-                o1 = ps_o.tile([P, 512], F32, name="o1_%d_%d" % (j, cp), tag="o1_%d" % cp)
-                mx_group(
-                    o1[:, 0:256], cj, sj, 1,
-                    lambda g: m1[:, 2 * g + cp, 0:256], lambda g: sm1[:, 2 * g + cp, 0:256],
+            o1 = [ps_o.tile([P, 512], F32, name="o1_%d_%d" % (j, cp), tag="o1_%d" % cp) for cp in range(2)]
+            o2 = [ps_o.tile([P, 512], F32, name="o2_%d_%d" % (j, cp), tag="o2_%d" % cp) for cp in range(2)]
+
+            def p_l0(g):
+                mx_pass(o0[:], cj, sj, 0, g, w0c[:, g, :], w0s[:, g, :])
+
+            def p_l1a(cp, g):
+                mx_pass(o1[cp][:, 0:256], cj, sj, 1, g, m1[:, 2 * g + cp, 0:256], sm1[:, 2 * g + cp, 0:256])
+
+            def p_l1b(cp, g):
+                mx_pass(o1[cp][:, 256:384], cj, sj, 2, g, m1[:, 2 * g + cp, 0:128], sm1[:, 2 * g + cp, 0:128])
+
+            def p_l2a(cp, g):
+                mx_pass(o2[cp][:, 0:128], cj, sj, 2, g, m2[:, 2 * g + cp, 128:256], sm2[:, 2 * g + cp, 128:256])
+
+            def p_l2b(cp, g):
+                mx_pass(o2[cp][:, 128:384], cj, sj, 3, g, m2[:, 2 * g + cp, 0:256], sm2[:, 2 * g + cp, 0:256])
+
+            def out_l0():
+                nc.scalar.activation(
+                    out=ost[:, :, 0:128], in_=o0[:].rearrange("p (c w) -> p c w", c=4), func=COPY, scale=ALPHA0
                 )
-                mx_group(
-                    o1[:, 256:384], cj, sj, 2,
-                    lambda g: m1[:, 2 * g + cp, 0:128], lambda g: sm1[:, 2 * g + cp, 0:128],
-                )
+
+            def out_l1(cp):
                 nc.scalar.activation(
                     out=ost[:, 2 * cp : 2 * cp + 2, 128:320].rearrange("p c (w i) -> p c w i", i=3),
-                    in_=o1[:, 0:384].rearrange("p (i c w) -> p c w i", i=3, c=2),
+                    in_=o1[cp][:, 0:384].rearrange("p (i c w) -> p c w i", i=3, c=2),
                     func=COPY,
                     scale=ALPHA1,
                 )
-            for cp in range(2):
-                o2 = ps_o.tile([P, 512], F32, name="o2_%d_%d" % (j, cp), tag="o2_%d" % cp)
-                mx_group(
-                    o2[:, 0:128], cj, sj, 2,
-                    lambda g: m2[:, 2 * g + cp, 128:256], lambda g: sm2[:, 2 * g + cp, 128:256],
-                )
-                mx_group(
-                    o2[:, 128:384], cj, sj, 3,
-                    lambda g: m2[:, 2 * g + cp, 0:256], lambda g: sm2[:, 2 * g + cp, 0:256],
-                )
+
+            def out_l2(cp):
                 nc.scalar.activation(
                     out=ost[:, 2 * cp : 2 * cp + 2, 320:480].rearrange("p c (w i) -> p c w i", i=5),
-                    in_=o2[:, 0:320].rearrange("p (i c w) -> p c w i", i=5, c=2),
+                    in_=o2[cp][:, 0:320].rearrange("p (i c w) -> p c w i", i=5, c=2),
                     func=COPY,
                     scale=ALPHA2,
                 )
-            nc.scalar.dma_start(out=out_view[j], in_=ost[:].rearrange("p c f -> p (c f)"))
+
+            if j < NJ - 1:
+                for g in range(4):
+                    p_l0(g)
+                out_l0()
+                for cp in range(2):
+                    for g in range(4):
+                        p_l1a(cp, g)
+                    for g in range(4):
+                        p_l1b(cp, g)
+                    out_l1(cp)
+                for cp in range(2):
+                    for g in range(4):
+                        p_l2a(cp, g)
+                    for g in range(4):
+                        p_l2b(cp, g)
+                    out_l2(cp)
+                nc.scalar.dma_start(out=out_view[j], in_=ost[:].rearrange("p c f -> p (c f)"))
+            else:
+                for g in range(4):
+                    p_l0(g)
+                    for cp in range(2):
+                        p_l1a(cp, g)
+                    for cp in range(2):
+                        p_l2b(cp, g)
+                out_l0()
+                nc.sync.dma_start(out=out_cols[j][:, :, 0:128], in_=ost[:, :, 0:128])
+                for cp in range(2):
+                    for g in range(4):
+                        p_l1b(cp, g)
+                    out_l1(cp)
+                nc.sync.dma_start(out=out_cols[j][:, :, 128:320], in_=ost[:, :, 128:320])
+                for cp in range(2):
+                    for g in range(4):
+                        p_l2a(cp, g)
+                    out_l2(cp)
+                nc.sync.dma_start(out=out_cols[j][:, :, 320:480], in_=ost[:, :, 320:480])
 
         def select_rows(ws, col, width, sel, rhs):
             nc.tensor.matmul(out=ws[:, col : col + width], lhsT=sel[:], rhs=rhs, start=True, stop=True)

@@ -22,7 +22,7 @@ FLOPS = 2 * NODES * (1 * 2048 * 512 + 3 * 1024 * 256 + 5 * 512 * 128)
 ALPHA0 = 1.0 / math.sqrt(2048.0)
 ALPHA1 = 1.0 / math.sqrt(1024.0)
 ALPHA2 = 1.0 / math.sqrt(512.0)
-POOL_PASSES = (2, 0, 3)
+POOL_PASS = 3
 
 
 def tile_tensorproductselfinteraction_kernel(tc, node_embeddings, Z_embeddings, W0, W1, W2, out):
@@ -153,8 +153,8 @@ def tile_tensorproductselfinteraction_kernel(tc, node_embeddings, Z_embeddings, 
                     stop=True,
                 )
             xtd[j] = xt
-            xs = xspool.tile([P, P], BF16, name="xs%d" % j, tag="xs")
-            nc.scalar.copy(out=xs[:], in_=xt[:, 768:1024].rearrange("p (q b) -> p q b", b=2)[:, :, 0])
+            xs = xspool.tile([P, 512], BF16, name="xs%d" % j, tag="xs")
+            nc.scalar.copy(out=xs[:], in_=xt[:].rearrange("p (q b) -> p q b", b=2)[:, :, 0])
             xsb[j] = xs
 
         def stage_b(j):
@@ -162,25 +162,22 @@ def tile_tensorproductselfinteraction_kernel(tc, node_embeddings, Z_embeddings, 
             xd = xtd[j]
             cj = cpool.tile([P, 4, 512], U32, name="cj%d" % j, tag="cj", align_bytes=64)
             sj = cpool.tile([P, 4, 512], U8, name="sj%d" % j, tag="sj", align_bytes=64)
-            for g in POOL_PASSES:
-                nc.gpsimd.tensor_tensor(
-                    out=prod[:, g, 1536:2048].rearrange("p (q t) -> p q t", t=4),
-                    in0=xsb[j][:].unsqueeze(2).to_broadcast([P, P, 4]),
-                    in1=zt[:, j % 2, :, 4 * g : 4 * g + 4],
-                    op=MULT,
-                )
+            nc.gpsimd.tensor_tensor(
+                out=prod[:, POOL_PASS, :].rearrange("p (T q t) -> p T q t", T=4, t=4),
+                in0=xsb[j][:].rearrange("p (T q) -> p T q", T=4).unsqueeze(3).to_broadcast([P, 4, P, 4]),
+                in1=zt[:, j % 2, :, 4 * POOL_PASS : 4 * POOL_PASS + 4].unsqueeze(1).to_broadcast([P, 4, P, 4]),
+                op=MULT,
+            )
             for g in range(4):
-                nt = 3 if g in POOL_PASSES else 4
+                if g == POOL_PASS:
+                    continue
                 nc.vector.tensor_tensor(
-                    out=prod[:, g, 0 : nt * 512].rearrange("p (T q a b) -> p T q a b", T=nt, q=P, a=2, b=2),
-                    in0=xd[:, 0 : nt * 256]
-                    .rearrange("p (T q b) -> p T q b", T=nt, b=2)
-                    .unsqueeze(3)
-                    .to_broadcast([P, nt, P, 2, 2]),
+                    out=prod[:, g, :].rearrange("p (T q a b) -> p T q a b", T=4, q=P, a=2, b=2),
+                    in0=xd[:].rearrange("p (T q b) -> p T q b", T=4, b=2).unsqueeze(3).to_broadcast([P, 4, P, 2, 2]),
                     in1=zt[:, j % 2, :, 4 * g : 4 * g + 4]
                     .rearrange("p q (a b) -> p q a b", a=2)
                     .unsqueeze(1)
-                    .to_broadcast([P, nt, P, 2, 2]),
+                    .to_broadcast([P, 4, P, 2, 2]),
                     op=MULT,
                 )
             if j < NJ - 1:
@@ -290,31 +287,35 @@ def tile_tensorproductselfinteraction_kernel(tc, node_embeddings, Z_embeddings, 
             nc.tensor.matmul(out=ws[:, col : col + width], lhsT=sel[:], rhs=rhs, start=True, stop=True)
 
         def prep_w0():
-            for g in range(4):
-                wg = wgpool.tile([P, 2048], BF16, name="wg0_%d" % g, tag="wg", align_bytes=64)
-                nc.scalar.copy(
-                    out=wg[:].rearrange("p (c i t) -> p c t i", i=4, t=4),
-                    in_=wraw0[:, 4 * g : 4 * g + 4, :].rearrange("p t (c i) -> p c t i", i=4),
-                )
-                nc.vector.quantize_mx(out=w0c[:, g, :].bitcast(FP8X4), scales=w0s[:, g, :], in_=wg[:])
-
-        def prep_w1():
-            for gp in range(2):
-                wg = wgpool.tile([P, 2048], BF16, name="wg1_%d" % gp, tag="wg", align_bytes=64)
+            for h in range(2):
+                wg = wgpool.tile([P, 4096], BF16, name="wg0_%d" % h, tag="wg", align_bytes=64)
                 for gg in range(2):
-                    g = 2 * gp + gg
-                    ws = ps_o.tile([P, 1024], BF16, name="ws1_%d" % g, tag="o2_%d" % gg)
-                    for t in range(4):
-                        select_rows(ws, t * 256, 256, sel1, wraw1[:, 4 * g + t, :])
+                    g = 2 * h + gg
                     nc.scalar.copy(
-                        out=wg[:, gg * 1024 : (gg + 1) * 1024].rearrange("p (w t) -> p w t", t=4),
-                        in_=ws[:].rearrange("p (t w) -> p w t", t=4),
+                        out=wg[:, gg * 2048 : (gg + 1) * 2048].rearrange("p (c i t) -> p c t i", i=4, t=4),
+                        in_=wraw0[:, 4 * g : 4 * g + 4, :].rearrange("p t (c i) -> p c t i", i=4),
                     )
                 nc.vector.quantize_mx(
-                    out=c1[:, 4 * gp : 4 * gp + 4, :].rearrange("p a c -> p (a c)").bitcast(FP8X4),
-                    scales=s1[:, 4 * gp : 4 * gp + 4, :].rearrange("p a c -> p (a c)"),
+                    out=w0c[:, 2 * h : 2 * h + 2, :].rearrange("p g c -> p (g c)").bitcast(FP8X4),
+                    scales=w0s[:, 2 * h : 2 * h + 2, :].rearrange("p g c -> p (g c)"),
                     in_=wg[:],
                 )
+
+        def prep_w1():
+            wg = wgpool.tile([P, 4096], BF16, name="wg1", tag="wg", align_bytes=64)
+            for g in range(4):
+                ws = ps_o.tile([P, 1024], BF16, name="ws1_%d" % g, tag="o2_%d" % (g % 2))
+                for t in range(4):
+                    select_rows(ws, t * 256, 256, sel1, wraw1[:, 4 * g + t, :])
+                nc.scalar.copy(
+                    out=wg[:, g * 1024 : (g + 1) * 1024].rearrange("p (w t) -> p w t", t=4),
+                    in_=ws[:].rearrange("p (t w) -> p w t", t=4),
+                )
+            nc.vector.quantize_mx(
+                out=c1[:].rearrange("p a c -> p (a c)").bitcast(FP8X4),
+                scales=s1[:].rearrange("p a c -> p (a c)"),
+                in_=wg[:],
+            )
             for h in range(2):
                 rows = slice(64 * h, 64 * h + 64)
                 nc.vector.tensor_copy(
@@ -325,7 +326,7 @@ def tile_tensorproductselfinteraction_kernel(tc, node_embeddings, Z_embeddings, 
                 )
 
         def prep_w2():
-            wg = wgpool.tile([P, 2048], BF16, name="wg2", tag="wg", align_bytes=64)
+            wg = wgpool.tile([P, 4096], BF16, name="wg2", tag="wg", align_bytes=64)
             for gp in range(2):
                 ws = ps_o.tile([P, 1024], BF16, name="ws2_%d" % gp, tag="o2_%d" % gp)
                 for b in range(2):
@@ -338,7 +339,7 @@ def tile_tensorproductselfinteraction_kernel(tc, node_embeddings, Z_embeddings, 
             nc.vector.quantize_mx(
                 out=c2[:].rearrange("p a c -> p (a c)").bitcast(FP8X4),
                 scales=s2[:].rearrange("p a c -> p (a c)"),
-                in_=wg[:],
+                in_=wg[:, 0:2048],
             )
             for r in range(4):
                 rows = slice(32 * r, 32 * r + 32)

@@ -22,7 +22,7 @@ FLOPS = 2 * NODES * (1 * 2048 * 512 + 3 * 1024 * 256 + 5 * 512 * 128)
 ALPHA0 = 1.0 / math.sqrt(2048.0)
 ALPHA1 = 1.0 / math.sqrt(1024.0)
 ALPHA2 = 1.0 / math.sqrt(512.0)
-POOL_PASS = 3
+POOL_FIRST_TILE = {0: 2, 1: 3}
 
 
 def tile_tensorproductselfinteraction_kernel(tc, node_embeddings, Z_embeddings, W0, W1, W2, out):
@@ -154,7 +154,7 @@ def tile_tensorproductselfinteraction_kernel(tc, node_embeddings, Z_embeddings, 
                 )
             xtd[j] = xt
             xs = xspool.tile([P, 512], BF16, name="xs%d" % j, tag="xs")
-            nc.scalar.copy(out=xs[:], in_=xt[:].rearrange("p (q b) -> p q b", b=2)[:, :, 0])
+            nc.scalar.copy(out=xs[:, 256:512], in_=xt[:, 512:1024].rearrange("p (q b) -> p q b", b=2)[:, :, 0])
             xsb[j] = xs
 
         def stage_b(j):
@@ -162,22 +162,29 @@ def tile_tensorproductselfinteraction_kernel(tc, node_embeddings, Z_embeddings, 
             xd = xtd[j]
             cj = cpool.tile([P, 4, 512], U32, name="cj%d" % j, tag="cj", align_bytes=64)
             sj = cpool.tile([P, 4, 512], U8, name="sj%d" % j, tag="sj", align_bytes=64)
-            nc.gpsimd.tensor_tensor(
-                out=prod[:, POOL_PASS, :].rearrange("p (T q t) -> p T q t", T=4, t=4),
-                in0=xsb[j][:].rearrange("p (T q) -> p T q", T=4).unsqueeze(3).to_broadcast([P, 4, P, 4]),
-                in1=zt[:, j % 2, :, 4 * POOL_PASS : 4 * POOL_PASS + 4].unsqueeze(1).to_broadcast([P, 4, P, 4]),
-                op=MULT,
-            )
+            for g in sorted(POOL_FIRST_TILE):
+                t0 = POOL_FIRST_TILE[g]
+                nc.gpsimd.tensor_tensor(
+                    out=prod[:, g, t0 * 512 : 2048].rearrange("p (T q t) -> p T q t", q=P, t=4),
+                    in0=xsb[j][:, t0 * P : 512]
+                    .rearrange("p (T q) -> p T q", q=P)
+                    .unsqueeze(3)
+                    .to_broadcast([P, 4 - t0, P, 4]),
+                    in1=zt[:, j % 2, :, 4 * g : 4 * g + 4].unsqueeze(1).to_broadcast([P, 4 - t0, P, 4]),
+                    op=MULT,
+                )
             for g in range(4):
-                if g == POOL_PASS:
-                    continue
+                nt = POOL_FIRST_TILE.get(g, 4)
                 nc.vector.tensor_tensor(
-                    out=prod[:, g, :].rearrange("p (T q a b) -> p T q a b", T=4, q=P, a=2, b=2),
-                    in0=xd[:].rearrange("p (T q b) -> p T q b", T=4, b=2).unsqueeze(3).to_broadcast([P, 4, P, 2, 2]),
+                    out=prod[:, g, 0 : nt * 512].rearrange("p (T q a b) -> p T q a b", T=nt, q=P, a=2, b=2),
+                    in0=xd[:, 0 : nt * 256]
+                    .rearrange("p (T q b) -> p T q b", T=nt, b=2)
+                    .unsqueeze(3)
+                    .to_broadcast([P, nt, P, 2, 2]),
                     in1=zt[:, j % 2, :, 4 * g : 4 * g + 4]
                     .rearrange("p q (a b) -> p q a b", a=2)
                     .unsqueeze(1)
-                    .to_broadcast([P, 4, P, 2, 2]),
+                    .to_broadcast([P, nt, P, 2, 2]),
                     op=MULT,
                 )
             if j < NJ - 1:

@@ -8,7 +8,6 @@ BF16 = mybir.dt.bfloat16
 F32 = mybir.dt.float32
 U32 = mybir.dt.uint32
 U8 = mybir.dt.uint8
-I32 = mybir.dt.int32
 FP8X4 = mybir.dt.float8_e4m3fn_x4
 COPY = mybir.ActivationFunctionType.Copy
 MULT = mybir.AluOpType.mult
@@ -17,69 +16,64 @@ P = 128
 NODES = 2048
 NJ = NODES // P
 FEAT = 480
+UNITS = 11
 FLOPS = 2 * NODES * (1 * 2048 * 512 + 3 * 1024 * 256 + 5 * 512 * 128)
 
 ALPHA0 = 1.0 / math.sqrt(2048.0)
 ALPHA1 = 1.0 / math.sqrt(1024.0)
 ALPHA2 = 1.0 / math.sqrt(512.0)
-POOL_FIRST_TILE = {0: 2, 1: 3}
 
 
 def tile_tensorproductselfinteraction_kernel(tc, node_embeddings, Z_embeddings, W0, W1, W2, out):
     nc = tc.nc
     x_view = node_embeddings.rearrange("(j q) f -> q j f", q=P)
+    z_nat_view = Z_embeddings.rearrange("(j q) v -> q j v", q=P)
     z_view = Z_embeddings.rearrange("(k n) v -> k (n v)", k=NJ // 2)
     out_view = out.rearrange("(j q c) f -> j q (c f)", q=P, c=4)
     out_cols = out.rearrange("(j q c) f -> j q c f", q=P, c=4)
+    w1_view = W1.rearrange("u v w -> (u v) w").rearrange("(G k e q a) w -> G k q e (a w)", G=2, k=2, e=2, q=64, a=2)
+    w2_view = W2.rearrange("u v w -> (u v) w").rearrange("(k e q a) w -> k q e (a w)", k=2, e=2, q=64, a=2)
 
     with ExitStack() as ctx:
+        ctx.enter_context(tc.manual_schedule())
         const = ctx.enter_context(tc.tile_pool(name="const", bufs=1))
         zpool = ctx.enter_context(tc.tile_pool(name="zpool", bufs=3))
-        xspool = ctx.enter_context(tc.tile_pool(name="xspool", bufs=3))
+        xpool = ctx.enter_context(tc.tile_pool(name="xpool", bufs=3))
         wgpool = ctx.enter_context(tc.tile_pool(name="wgpool", bufs=2))
-        cpool = ctx.enter_context(tc.tile_pool(name="cpool", bufs=5))
+        npool = ctx.enter_context(tc.tile_pool(name="npool", bufs=2))
+        ppool = ctx.enter_context(tc.tile_pool(name="ppool", bufs=2))
+        cpool = ctx.enter_context(tc.tile_pool(name="cpool", bufs=3))
         opool = ctx.enter_context(tc.tile_pool(name="opool", bufs=3))
+        ps_x = ctx.enter_context(tc.psum_pool(name="ps_x", bufs=1))
         ps_t = ctx.enter_context(tc.psum_pool(name="ps_t", bufs=3))
         ps_o = ctx.enter_context(tc.psum_pool(name="ps_o", bufs=1))
 
         ident = const.tile([P, P], BF16, name="ident")
-        make_identity(nc, ident[:])
-        idup = const.tile([P, P, 2], BF16, name="idup")
-        sel1 = const.tile([P, P], BF16, name="sel1")
-        sel2 = const.tile([P, P], BF16, name="sel2")
-
+        identf = const.tile([P, P], F32, name="identf")
+        ident4 = const.tile([P, P, 4], BF16, name="ident4")
+        sel0 = const.tile([P, P], BF16, name="sel0")
+        selb = const.tile([P, P], BF16, name="selb")
+        zn = const.tile([P, NJ, 16], BF16, name="zn")
+        xn = [const.tile([P, 4, FEAT], BF16, name="xn%d" % c) for c in range(4)]
+        raw0 = const.tile([P, 16, 512], BF16, name="raw0")
+        raw1 = const.tile([P, 2, 2, 2, 256], BF16, name="raw1")
+        raw2 = const.tile([P, 2, 2, 128], BF16, name="raw2")
         w0c = const.tile([P, 4, 512], U32, name="w0c", align_bytes=64)
         w0s = const.tile([P, 4, 512], U8, name="w0s", align_bytes=64)
-        c1 = const.tile([P, 8, 128], U32, name="c1", align_bytes=64)
-        s1 = const.tile([P, 8, 128], U8, name="s1", align_bytes=64)
-        c2 = const.tile([P, 8, 64], U32, name="c2", align_bytes=64)
-        s2 = const.tile([P, 8, 64], U8, name="s2", align_bytes=64)
-        m1 = const.tile([P, 8, 256], U32, name="m1", align_bytes=64)
-        sm1 = const.tile([P, 8, 256], U8, name="sm1", align_bytes=64)
-        m2 = const.tile([P, 8, 256], U32, name="m2", align_bytes=64)
-        sm2 = const.tile([P, 8, 256], U8, name="sm2", align_bytes=64)
+        w1c = const.tile([P, 2, 256], U32, name="w1c", align_bytes=64)
+        w1s = const.tile([P, 2, 256], U8, name="w1s", align_bytes=64)
+        w2c = const.tile([P, 128], U32, name="w2c", align_bytes=64)
+        w2s = const.tile([P, 128], U8, name="w2s", align_bytes=64)
 
-        wraw0 = const.tile([P, 16, 512], BF16, name="wraw0")
-        wraw1 = const.tile([P, 16, 256], BF16, name="wraw1")
-        wraw2 = const.tile([P, 16, 128], BF16, name="wraw2")
-        xn = [const.tile([P, 4, FEAT], BF16, name="xn%d" % c) for c in range(4)]
-        xa = [const.tile([P, 512], BF16, name="xa%d" % k) for k in range(4)]
-        prod = const.tile([P, 4, 2048], BF16, name="prod", align_bytes=64)
-
-        nc.gpsimd.memset(m1[:].bitcast(F32), 0.0)
-        nc.gpsimd.memset(m2[:].bitcast(F32), 0.0)
-        nc.vector.memset(s1[:].bitcast(I32), 0)
-        nc.vector.memset(s2[:].bitcast(I32), 0)
-        for k in range(4):
-            nc.vector.memset(xa[k][:, FEAT:512].bitcast(I32), 0)
+        make_identity(nc, ident[:])
+        make_identity(nc, identf[:])
 
         zb = {}
 
         def load_z(k):
             zt = zpool.tile([P, 2, P, 16], BF16, name="zb%d" % k, tag="zb")
             nc.sync.dma_start(
-                out=zt[:].rearrange("p j q v -> p (j q v)"),
-                in_=z_view[k].partition_broadcast(P),
+                out=zt[:].rearrange("p j q v -> p (j q v)"), in_=z_view[k].partition_broadcast(P)
             )
             zb[k] = zt
 
@@ -87,289 +81,324 @@ def tile_tensorproductselfinteraction_kernel(tc, node_embeddings, Z_embeddings, 
             nc.sync.dma_start(out=xn[c][:], in_=x_view[:, 4 * c : 4 * c + 4, :])
 
         nc.sync.dma_start(out=xn[0][:, 0:1, :], in_=x_view[:, 0:1, :])
-        z0 = zpool.tile([P, 2, P, 16], BF16, name="zb0", tag="zb")
-        zb[0] = z0
-        for jj in range(2):
-            nc.scalar.dma_start(
-                out=z0[:, jj, :, :].rearrange("p q v -> p (q v)"),
-                in_=z_view[0][jj * 2048 : (jj + 1) * 2048].partition_broadcast(P),
-            )
-            if jj == 0:
-                nc.sync.dma_start(out=xn[0][:, 1:4, :], in_=x_view[:, 1:4, :])
-        for cc in range(4):
-            for e in range(2):
+        nc.scalar.dma_start(out=zn[:], in_=z_nat_view)
+        nc.sync.dma_start(out=xn[0][:, 1:4, :], in_=x_view[:, 1:4, :])
+        for G in range(2):
+            for k in range(2):
                 nc.sync.dma_start(
-                    out=wraw0[32 * cc + e : 32 * cc + 32 : 2, :, :], in_=W0[2 * cc + e : P : 8, :, :]
+                    out=raw1[64 * k : 64 * k + 64, G, :, :, :].rearrange("q e a w -> q e (a w)"), in_=w1_view[G, k]
                 )
-        for h in range(2):
-            nc.sync.dma_start(out=wraw1[64 * h : 64 * h + 64, :, :], in_=W1)
-        for r in range(4):
-            nc.sync.dma_start(out=wraw2[32 * r : 32 * r + 32, :, :], in_=W2)
-        load_z(1)
+        for k in range(2):
+            nc.sync.dma_start(
+                out=raw2[64 * k : 64 * k + 64, :, :, :].rearrange("q e a w -> q e (a w)"), in_=w2_view[k]
+            )
+        load_z(0)
+        for g in range(4):
+            nc.sync.dma_start(out=raw0[:, 4 * g : 4 * g + 4, :], in_=W0[:, 4 * g : 4 * g + 4, :])
         load_x(1)
-        load_z(2)
+        load_z(1)
         load_x(2)
+        load_z(2)
         load_x(3)
 
-        nc.vector.tensor_copy(out=idup[:], in_=ident[:].unsqueeze(2).to_broadcast([P, P, 2]))
-        for h in range(2):
-            nc.vector.tensor_copy(
-                out=sel1[:, 64 * h : 64 * h + 64].rearrange("k (G s a) -> k G s a", G=2, s=8, a=4),
-                in_=ident[:, 0:64].rearrange("k (G a s) -> k G s a", G=2, a=4, s=8),
-            )
-        for r in range(4):
-            nc.vector.tensor_copy(
-                out=sel2[:, 32 * r : 32 * r + 32].rearrange("k (s a) -> k s a", s=8, a=4),
-                in_=ident[:, 0:32].rearrange("k (a s) -> k s a", a=4, s=8),
-            )
+        nc.vector.tensor_copy(out=ident4[:], in_=ident[:].unsqueeze(2).to_broadcast([P, P, 4]))
+        nc.vector.tensor_copy(
+            out=sel0[:].rearrange("k (c A e) -> k c A e", c=4, A=16, e=2),
+            in_=ident[:].rearrange("k (A c e) -> k c A e", A=16, c=4, e=2),
+        )
+        for d in range(2):
+            for b in range(2):
+                nc.vector.tensor_copy(
+                    out=selb[:].rearrange("k (h c l b d) -> k b d h c l", h=4, c=4, l=2, b=2, d=2)[:, b, d],
+                    in_=ident[:].rearrange("k (d c b h l) -> k d b h c l", d=2, c=4, b=2, h=4, l=2)[:, d, b],
+                )
 
+        xp = {}
         xtd = {}
-        xsb = {}
+        pn = {}
+        pt = {}
+        p0 = {}
         codes = {}
+        banks = {}
+        accs = {}
+        osts = {}
 
-        def stage_a(j):
-            src = xn[j // 4]
-            jj = j % 4
-            dst = xa[j % 4]
+        def permute(j):
+            src = xn[j // 4][:, j % 4, :]
+            dst = xpool.tile([P, FEAT], BF16, name="xp%d" % j, tag="xp")
+            xp[j] = dst
             nc.scalar.copy(
                 out=dst[:, 0:128].rearrange("p (c A e) -> p c A e", c=4, A=16, e=2),
-                in_=src[:, jj, 0:128].rearrange("p (A c e) -> p c A e", A=16, c=4, e=2),
+                in_=src[:, 0:128].rearrange("p (A c e) -> p c A e", A=16, c=4, e=2),
             )
-            d1 = dst[:, 128:320].rearrange("p (i G s a) -> p i G s a", i=3, G=2, s=8, a=4)
-            r1 = src[:, jj, 128:320].rearrange("p (G a s i) -> p i G s a", G=2, a=4, s=8, i=3)
+            units = dst[:, 128:480].rearrange("p (r s m) -> p r s m", r=UNITS, s=8, m=4)
+            l1 = src[:, 128:320].rearrange("p (G m s i) -> p G i s m", G=2, m=4, s=8, i=3)
+            l2 = src[:, 320:480].rearrange("p (m s i) -> p i s m", m=4, s=8, i=5)
             for G in range(2):
-                nc.scalar.copy(out=d1[:, :, G, :, :], in_=r1[:, :, G, :, :])
-            nc.scalar.copy(
-                out=dst[:, 320:480].rearrange("p (i s a) -> p i s a", i=5, s=8, a=4),
-                in_=src[:, jj, 320:480].rearrange("p (a s i) -> p i s a", a=4, s=8, i=5),
+                nc.scalar.copy(out=units[:, 3 * G : 3 * G + 3], in_=l1[:, G])
+            nc.scalar.copy(out=units[:, 6:11], in_=l2)
+
+        def transpose_x0(j):
+            xt = ps_x.tile([P, 512], BF16, name="xt%d" % j, tag="xt")
+            nc.tensor.matmul(
+                out=xt[:], lhsT=xp[j][:, 0:128], rhs=ident4[:].rearrange("p q b -> p (q b)"), start=True, stop=True
             )
-            xt = ps_t.tile([P, 1024], BF16, name="xt%d" % j, tag="tp")
-            for T in range(4):
-                nc.tensor.matmul(
-                    out=xt[:, T * 256 : (T + 1) * 256],
-                    lhsT=dst[:, T * P : (T + 1) * P],
-                    rhs=idup[:].rearrange("p q b -> p (q b)"),
-                    start=True,
-                    stop=True,
-                )
             xtd[j] = xt
-            xs = xspool.tile([P, 512], BF16, name="xs%d" % j, tag="xs")
-            nc.scalar.copy(out=xs[:, 256:512], in_=xt[:, 512:1024].rearrange("p (q b) -> p q b", b=2)[:, :, 0])
-            xsb[j] = xs
 
-        def stage_b(j):
-            zt = zb[j // 2]
-            xd = xtd[j]
-            cj = cpool.tile([P, 4, 512], U32, name="cj%d" % j, tag="cj", align_bytes=64)
-            sj = cpool.tile([P, 4, 512], U8, name="sj%d" % j, tag="sj", align_bytes=64)
-            for g in sorted(POOL_FIRST_TILE):
-                t0 = POOL_FIRST_TILE[g]
-                nc.gpsimd.tensor_tensor(
-                    out=prod[:, g, t0 * 512 : 2048].rearrange("p (T q t) -> p T q t", q=P, t=4),
-                    in0=xsb[j][:, t0 * P : 512]
-                    .rearrange("p (T q) -> p T q", q=P)
-                    .unsqueeze(3)
-                    .to_broadcast([P, 4 - t0, P, 4]),
-                    in1=zt[:, j % 2, :, 4 * g : 4 * g + 4].unsqueeze(1).to_broadcast([P, 4 - t0, P, 4]),
-                    op=MULT,
+        def product_l0(j):
+            prod = ppool.tile([P, 4, 512], BF16, name="p0_%d" % j, tag="p0", align_bytes=64)
+            nc.vector.tensor_tensor(
+                out=prod[:].rearrange("p g (q t) -> p g q t", t=4),
+                in0=xtd[j][:].rearrange("p (q t) -> p q t", t=4).unsqueeze(1).to_broadcast([P, 4, P, 4]),
+                in1=zb[j // 2][:, j % 2, :, :].rearrange("p q (g t) -> p g q t", g=4),
+                op=MULT,
+            )
+            p0[j] = prod
+
+        def product_units(j, vs):
+            if j not in pn:
+                pn[j] = npool.tile([P, UNITS, 512], BF16, name="pn%d" % j, tag="pn", align_bytes=64)
+            view = pn[j][:].rearrange("p r (a h c l s) -> p a h l c r s", a=2, h=4, c=4, l=2, s=8)
+            for v in vs:
+                nc.vector.tensor_scalar(
+                    out=view[:, v % 2, v // 4, (v // 2) % 2],
+                    in0=xp[j][:, 128:480].rearrange("p (r c s) -> p c r s", r=UNITS, c=4, s=8),
+                    scalar1=zn[:, j, v : v + 1],
+                    scalar2=None,
+                    op0=MULT,
                 )
-            for g in range(4):
-                nt = POOL_FIRST_TILE.get(g, 4)
-                nc.vector.tensor_tensor(
-                    out=prod[:, g, 0 : nt * 512].rearrange("p (T q a b) -> p T q a b", T=nt, q=P, a=2, b=2),
-                    in0=xd[:, 0 : nt * 256]
-                    .rearrange("p (T q b) -> p T q b", T=nt, b=2)
-                    .unsqueeze(3)
-                    .to_broadcast([P, nt, P, 2, 2]),
-                    in1=zt[:, j % 2, :, 4 * g : 4 * g + 4]
-                    .rearrange("p q (a b) -> p q a b", a=2)
-                    .unsqueeze(1)
-                    .to_broadcast([P, nt, P, 2, 2]),
-                    op=MULT,
-                )
-            if j < NJ - 1:
-                for h in range(2):
-                    nc.vector.quantize_mx(
-                        out=cj[:, 2 * h : 2 * h + 2, :].rearrange("p g c -> p (g c)").bitcast(FP8X4),
-                        scales=sj[:, 2 * h : 2 * h + 2, :].rearrange("p g c -> p (g c)"),
-                        in_=prod[:, 2 * h : 2 * h + 2, :].rearrange("p g c -> p (g c)"),
+
+        def transposes(j, b):
+            tp = ps_t.tile([P, 512], F32, name="tp%d_%d" % (j, b), tag="tp")
+            for r in range(2 * b, min(2 * b + 2, UNITS)):
+                for a in range(2):
+                    col = (2 * (r - 2 * b) + a) * P
+                    nc.tensor.transpose(
+                        tp[:, col : col + P], pn[j][:, r, a * 256 : (a + 1) * 256].bitcast(F32), identf[:]
                     )
-            else:
-                for g in range(4):
-                    nc.vector.quantize_mx(out=cj[:, g, :].bitcast(FP8X4), scales=sj[:, g, :], in_=prod[:, g, :])
-            codes[j] = (cj, sj)
+            banks[(j, b)] = tp
 
-        def mx_pass(acc, cj, sj, T, g, rhs, rhs_scale):
+        def copy_bank(j, b, engine_copy):
+            if j not in pt:
+                pt[j] = ppool.tile([P, UNITS, 512], BF16, name="pt%d" % j, tag="pt", align_bytes=64)
+            n = min(2, UNITS - 2 * b)
+            engine_copy(
+                out=pt[j][:, 2 * b : 2 * b + n, :].bitcast(F32).rearrange("p r (n a) -> p r n a", a=2),
+                in_=banks[(j, b)][:, 0 : 256 * n].rearrange("p (r a n) -> p r n a", r=n, a=2),
+            )
+
+        def code_tiles(j):
+            if j not in codes:
+                cj = cpool.tile([P, 15, P], U32, name="cj%d" % j, tag="cj", align_bytes=64)
+                sj = cpool.tile([P, 15, P], U8, name="sj%d" % j, tag="sj", align_bytes=64)
+                codes[j] = (cj, sj)
+            return codes[j]
+
+        def quantize_l0(j):
+            cj, sj = code_tiles(j)
+            nc.vector.quantize_mx(
+                out=cj[:, 0:4, :].rearrange("p g c -> p (g c)").bitcast(FP8X4),
+                scales=sj[:, 0:4, :].rearrange("p g c -> p (g c)"),
+                in_=p0[j][:].rearrange("p g c -> p (g c)"),
+            )
+
+        def quantize_units(j, r0, n):
+            cj, sj = code_tiles(j)
+            nc.vector.quantize_mx(
+                out=cj[:, 4 + r0 : 4 + r0 + n, :].rearrange("p g c -> p (g c)").bitcast(FP8X4),
+                scales=sj[:, 4 + r0 : 4 + r0 + n, :].rearrange("p g c -> p (g c)"),
+                in_=pt[j][:, r0 : r0 + n, :].rearrange("p g c -> p (g c)"),
+            )
+
+        def mx(acc, j, unit, rhs, rhs_scale, start, stop):
+            cj, sj = codes[j]
             nc.tensor.matmul_mx(
                 out=acc,
-                lhsT=cj[:, g, T * P : (T + 1) * P].bitcast(FP8X4),
-                lhsT_scale=sj[:, g, T * P : (T + 1) * P],
+                lhsT=cj[:, unit, :].bitcast(FP8X4),
+                lhsT_scale=sj[:, unit, :],
                 rhs=rhs.bitcast(FP8X4),
                 rhs_scale=rhs_scale,
-                start=(g == 0),
-                stop=(g == 3),
+                start=start,
+                stop=stop,
             )
 
-        def stage_c(j):
-            cj, sj = codes[j]
-            ost = opool.tile([P, 4, FEAT], F32, name="ost%d" % j, tag="ost")
-            o0 = ps_o.tile([P, 512], F32, name="o0_%d" % j, tag="o0")
-            o1 = [ps_o.tile([P, 512], F32, name="o1_%d_%d" % (j, cp), tag="o1_%d" % cp) for cp in range(2)]
-            o2 = [ps_o.tile([P, 512], F32, name="o2_%d_%d" % (j, cp), tag="o2_%d" % cp) for cp in range(2)]
+        def multiply(j, b):
+            acc = ps_o.tile([P, 512], F32, name="o%d_%d" % (j, b), tag="o%d" % b)
+            accs[(j, b)] = acc
+            l0_col = 384 if b < 2 else 320
+            for g in range(4):
+                mx(acc[:, l0_col : l0_col + P], j, g, w0c[:, g, b * P : (b + 1) * P], w0s[:, g, b * P : (b + 1) * P], g == 0, g == 3)
+            cp = b % 2
+            if b < 2:
+                for i in range(3):
+                    for G in range(2):
+                        mx(
+                            acc[:, i * P : (i + 1) * P],
+                            j,
+                            4 + G * 3 + i,
+                            w1c[:, G, cp * P : (cp + 1) * P],
+                            w1s[:, G, cp * P : (cp + 1) * P],
+                            G == 0,
+                            G == 1,
+                        )
+            else:
+                for i in range(5):
+                    mx(
+                        acc[:, i * 64 : (i + 1) * 64],
+                        j,
+                        10 + i,
+                        w2c[:, cp * 64 : (cp + 1) * 64],
+                        w2s[:, cp * 64 : (cp + 1) * 64],
+                        True,
+                        True,
+                    )
 
-            def p_l0(g):
-                mx_pass(o0[:], cj, sj, 0, g, w0c[:, g, :], w0s[:, g, :])
-
-            def p_l1a(cp, g):
-                mx_pass(o1[cp][:, 0:256], cj, sj, 1, g, m1[:, 2 * g + cp, 0:256], sm1[:, 2 * g + cp, 0:256])
-
-            def p_l1b(cp, g):
-                mx_pass(o1[cp][:, 256:384], cj, sj, 2, g, m1[:, 2 * g + cp, 0:128], sm1[:, 2 * g + cp, 0:128])
-
-            def p_l2a(cp, g):
-                mx_pass(o2[cp][:, 0:128], cj, sj, 2, g, m2[:, 2 * g + cp, 128:256], sm2[:, 2 * g + cp, 128:256])
-
-            def p_l2b(cp, g):
-                mx_pass(o2[cp][:, 128:384], cj, sj, 3, g, m2[:, 2 * g + cp, 0:256], sm2[:, 2 * g + cp, 0:256])
-
-            def out_l0():
-                nc.scalar.activation(
-                    out=ost[:, :, 0:128], in_=o0[:].rearrange("p (c w) -> p c w", c=4), func=COPY, scale=ALPHA0
-                )
-
-            def out_l1(cp):
+        def evacuate(j, b):
+            if j not in osts:
+                osts[j] = opool.tile([P, 4, FEAT], F32, name="ost%d" % j, tag="ost")
+            ost = osts[j]
+            acc = accs[(j, b)]
+            cp = b % 2
+            l0_col = 384 if b < 2 else 320
+            nc.scalar.activation(out=ost[:, b, 0:128], in_=acc[:, l0_col : l0_col + P], func=COPY, scale=ALPHA0)
+            if b < 2:
                 nc.scalar.activation(
                     out=ost[:, 2 * cp : 2 * cp + 2, 128:320].rearrange("p c (w i) -> p c w i", i=3),
-                    in_=o1[cp][:, 0:384].rearrange("p (i c w) -> p c w i", i=3, c=2),
+                    in_=acc[:, 0:384].rearrange("p (i c w) -> p c w i", i=3, c=2),
                     func=COPY,
                     scale=ALPHA1,
                 )
-
-            def out_l2(cp):
+            else:
                 nc.scalar.activation(
                     out=ost[:, 2 * cp : 2 * cp + 2, 320:480].rearrange("p c (w i) -> p c w i", i=5),
-                    in_=o2[cp][:, 0:320].rearrange("p (i c w) -> p c w i", i=5, c=2),
+                    in_=acc[:, 0:320].rearrange("p (i c w) -> p c w i", i=5, c=2),
                     func=COPY,
                     scale=ALPHA2,
                 )
 
-            if j < NJ - 1:
-                for g in range(4):
-                    p_l0(g)
-                out_l0()
-                for cp in range(2):
-                    for g in range(4):
-                        p_l1a(cp, g)
-                    for g in range(4):
-                        p_l1b(cp, g)
-                    out_l1(cp)
-                for cp in range(2):
-                    for g in range(4):
-                        p_l2a(cp, g)
-                    for g in range(4):
-                        p_l2b(cp, g)
-                    out_l2(cp)
-                nc.scalar.dma_start(out=out_view[j], in_=ost[:].rearrange("p c f -> p (c f)"))
-            else:
-                for g in range(4):
-                    p_l0(g)
-                    for cp in range(2):
-                        p_l1a(cp, g)
-                    for cp in range(2):
-                        p_l2b(cp, g)
-                out_l0()
-                nc.sync.dma_start(out=out_cols[j][:, :, 0:128], in_=ost[:, :, 0:128])
-                for cp in range(2):
-                    for g in range(4):
-                        p_l1b(cp, g)
-                    out_l1(cp)
-                nc.sync.dma_start(out=out_cols[j][:, :, 128:320], in_=ost[:, :, 128:320])
-                for cp in range(2):
-                    for g in range(4):
-                        p_l2a(cp, g)
-                    out_l2(cp)
-                nc.sync.dma_start(out=out_cols[j][:, :, 320:480], in_=ost[:, :, 320:480])
+        wg = {}
+        wsn = []
 
-        def select_rows(ws, col, width, sel, rhs):
-            nc.tensor.matmul(out=ws[:, col : col + width], lhsT=sel[:], rhs=rhs, start=True, stop=True)
+        def weight_bank(sel, rhs_of_pair, width):
+            wsn.append(0)
+            ws = ps_t.tile([P, 1024], BF16, name="ws%d" % len(wsn), tag="tp")
+            for b in range(2):
+                nc.tensor.matmul(
+                    out=ws[:, 0 : 4 * width].rearrange("p (w b e) -> p b w e", b=2, e=2)[:, b],
+                    lhsT=sel[:],
+                    rhs=rhs_of_pair(b),
+                    start=True,
+                    stop=True,
+                )
+            return ws
 
-        def prep_w0():
+        def weights_l0(g, engine_copy):
+            if g % 2 == 0:
+                wg[g // 2] = wgpool.tile([P, 4096], BF16, name="wg0_%d" % (g // 2), tag="wg", align_bytes=64)
             for h in range(2):
-                wg = wgpool.tile([P, 4096], BF16, name="wg0_%d" % h, tag="wg", align_bytes=64)
-                for gg in range(2):
-                    g = 2 * h + gg
-                    nc.scalar.copy(
-                        out=wg[:, gg * 2048 : (gg + 1) * 2048].rearrange("p (c i t) -> p c t i", i=4, t=4),
-                        in_=wraw0[:, 4 * g : 4 * g + 4, :].rearrange("p t (c i) -> p c t i", i=4),
-                    )
-                nc.vector.quantize_mx(
-                    out=w0c[:, 2 * h : 2 * h + 2, :].rearrange("p g c -> p (g c)").bitcast(FP8X4),
-                    scales=w0s[:, 2 * h : 2 * h + 2, :].rearrange("p g c -> p (g c)"),
-                    in_=wg[:],
+                ws = weight_bank(
+                    sel0,
+                    lambda b: raw0[:, 4 * g + 2 * b : 4 * g + 2 * b + 2, 256 * h : 256 * h + 256].rearrange("k e w -> k w e"),
+                    256,
                 )
+                o = (g % 2) * 2048 + h * 1024
+                engine_copy(out=wg[g // 2][:, o : o + 1024], in_=ws[:])
 
-        def prep_w1():
-            wg = wgpool.tile([P, 4096], BF16, name="wg1", tag="wg", align_bytes=64)
-            for g in range(4):
-                ws = ps_o.tile([P, 1024], BF16, name="ws1_%d" % g, tag="o2_%d" % (g % 2))
-                for t in range(4):
-                    select_rows(ws, t * 256, 256, sel1, wraw1[:, 4 * g + t, :])
-                nc.scalar.copy(
-                    out=wg[:, g * 1024 : (g + 1) * 1024].rearrange("p (w t) -> p w t", t=4),
-                    in_=ws[:].rearrange("p (t w) -> p w t", t=4),
-                )
+        def quantize_w0(h):
             nc.vector.quantize_mx(
-                out=c1[:].rearrange("p a c -> p (a c)").bitcast(FP8X4),
-                scales=s1[:].rearrange("p a c -> p (a c)"),
-                in_=wg[:],
+                out=w0c[:, 2 * h : 2 * h + 2, :].rearrange("p g c -> p (g c)").bitcast(FP8X4),
+                scales=w0s[:, 2 * h : 2 * h + 2, :].rearrange("p g c -> p (g c)"),
+                in_=wg[h][:],
             )
-            for h in range(2):
-                rows = slice(64 * h, 64 * h + 64)
-                nc.vector.tensor_copy(
-                    out=m1[rows, :, 128 * h : 128 * h + 128].bitcast(I32), in_=c1[rows, :, :].bitcast(I32)
-                )
-                nc.vector.tensor_copy(
-                    out=sm1[:].bitcast(I32)[:, :, 32 * h : 32 * h + 32], in_=s1[:].bitcast(I32)
-                )
 
-        def prep_w2():
-            wg = wgpool.tile([P, 4096], BF16, name="wg2", tag="wg", align_bytes=64)
-            for gp in range(2):
-                ws = ps_o.tile([P, 1024], BF16, name="ws2_%d" % gp, tag="o2_%d" % gp)
-                for b in range(2):
-                    for t in range(4):
-                        select_rows(ws, (b * 4 + t) * 128, 128, sel2, wraw2[:, 4 * (2 * gp + b) + t, :])
-                nc.scalar.copy(
-                    out=wg[:, gp * 1024 : (gp + 1) * 1024].rearrange("p (b w t) -> p b w t", b=2, t=4),
-                    in_=ws[:].rearrange("p (b t w) -> p b w t", b=2, t=4),
-                )
+        def weights_l12(engine_copy):
+            wg[2] = wgpool.tile([P, 4096], BF16, name="wg12", tag="wg", align_bytes=64)
+            for G in range(2):
+                ws = weight_bank(selb, lambda a: raw1[:, G, :, a, :].rearrange("k e w -> k w e"), 256)
+                engine_copy(out=wg[2][:, G * 1024 : (G + 1) * 1024], in_=ws[:])
+            ws = weight_bank(selb, lambda a: raw2[:, :, a, :].rearrange("k e w -> k w e"), 128)
+            engine_copy(out=wg[2][:, 2048:2560], in_=ws[:, 0:512])
+
+        def quantize_w12():
             nc.vector.quantize_mx(
-                out=c2[:].rearrange("p a c -> p (a c)").bitcast(FP8X4),
-                scales=s2[:].rearrange("p a c -> p (a c)"),
-                in_=wg[:, 0:2048],
+                out=w1c[:].rearrange("p g c -> p (g c)").bitcast(FP8X4),
+                scales=w1s[:].rearrange("p g c -> p (g c)"),
+                in_=wg[2][:, 0:2048],
             )
-            for r in range(4):
-                rows = slice(32 * r, 32 * r + 32)
-                nc.vector.tensor_copy(
-                    out=m2[rows, :, 64 * r : 64 * r + 64].bitcast(I32), in_=c2[rows, :, :].bitcast(I32)
-                )
-                nc.vector.tensor_copy(
-                    out=sm2[:].bitcast(I32)[:, :, 16 * r : 16 * r + 16], in_=s2[:].bitcast(I32)
-                )
+            nc.vector.quantize_mx(out=w2c[:].bitcast(FP8X4), scales=w2s[:], in_=wg[2][:, 2048:2560])
 
-        stage_a(0)
-        stage_a(1)
-        stage_b(0)
-        prep_w0()
-        stage_a(2)
-        stage_b(1)
-        prep_w1()
-        prep_w2()
-        for j in range(NJ):
-            if j + 3 < NJ:
-                stage_a(j + 3)
-            if j + 2 < NJ:
-                if (j + 2) % 2 == 0 and (j + 2) // 2 + 2 < NJ // 2:
-                    load_z((j + 2) // 2 + 2)
-                stage_b(j + 2)
-            stage_c(j)
+        scopy = nc.scalar.copy
+        vcopy = nc.vector.tensor_copy
+
+        def copy_engine(b):
+            return vcopy if b in {5} else scopy
+
+        permute(0)
+        permute(1)
+        transpose_x0(0)
+        product_units(0, range(16))
+        for b in range(3):
+            transposes(0, b)
+            copy_bank(0, b, scopy)
+        permute(2)
+        product_units(1, range(0, 8))
+        quantize_units(0, 0, 4)
+        for b in range(3, 6):
+            transposes(0, b)
+            copy_bank(0, b, scopy)
+        product_l0(0)
+        transpose_x0(1)
+        product_units(1, range(8, 16))
+        quantize_units(0, 4, 4)
+        quantize_units(0, 8, 2)
+        quantize_units(0, 10, 1)
+        weights_l12(scopy)
+        for g in range(4):
+            weights_l0(g, scopy)
+        quantize_l0(0)
+        quantize_w12()
+        quantize_w0(0)
+        quantize_w0(1)
+
+        for i in range(NJ):
+            n1 = i + 1 < NJ
+            n2 = i + 2 < NJ
+            if i > 0:
+                quantize_units(i, 8, 2)
+                quantize_units(i, 10, 1)
+            if n1:
+                for b in range(3):
+                    transposes(i + 1, b)
+                    copy_bank(i + 1, b, copy_engine(b))
+            if n2:
+                product_units(i + 2, range(0, 4))
+            if n1:
+                product_l0(i + 1)
+            if n2:
+                product_units(i + 2, range(4, 8))
+            for b in range(2):
+                multiply(i, b)
+                evacuate(i, b)
+            if n1:
+                quantize_l0(i + 1)
+            if n2:
+                product_units(i + 2, range(8, 12))
+            if n1:
+                quantize_units(i + 1, 0, 4)
+            if n2:
+                transpose_x0(i + 2)
+                product_units(i + 2, range(12, 16))
+            if n1:
+                for b in range(3, 6):
+                    transposes(i + 1, b)
+                    copy_bank(i + 1, b, copy_engine(b))
+            for b in range(2, 4):
+                multiply(i, b)
+                evacuate(i, b)
+            if n1:
+                quantize_units(i + 1, 4, 4)
+            if i + 3 < NJ:
+                permute(i + 3)
+            if (i + 2) % 2 == 0 and (i + 2) // 2 + 2 < NJ // 2:
+                load_z((i + 2) // 2 + 2)
+            nc.sync.dma_start(out=out_view[i], in_=osts[i][:].rearrange("p c f -> p (c f)"))

@@ -35,17 +35,15 @@ def tile_tensorproductselfinteraction_kernel(tc, node_embeddings, Z_embeddings, 
     w2_view = W2.rearrange("u v w -> (u v) w").rearrange("(k e q a) w -> k q e (a w)", k=2, e=2, q=64, a=2)
 
     with ExitStack() as ctx:
-        ctx.enter_context(tc.manual_schedule())
         const = ctx.enter_context(tc.tile_pool(name="const", bufs=1))
         zpool = ctx.enter_context(tc.tile_pool(name="zpool", bufs=3))
-        xpool = ctx.enter_context(tc.tile_pool(name="xpool", bufs=3))
+        xpool = ctx.enter_context(tc.tile_pool(name="xpool", bufs=4))
         wgpool = ctx.enter_context(tc.tile_pool(name="wgpool", bufs=2))
         npool = ctx.enter_context(tc.tile_pool(name="npool", bufs=2))
         ppool = ctx.enter_context(tc.tile_pool(name="ppool", bufs=2))
-        cpool = ctx.enter_context(tc.tile_pool(name="cpool", bufs=3))
+        cpool = ctx.enter_context(tc.tile_pool(name="cpool", bufs=4))
         opool = ctx.enter_context(tc.tile_pool(name="opool", bufs=3))
-        ps_x = ctx.enter_context(tc.psum_pool(name="ps_x", bufs=1))
-        ps_t = ctx.enter_context(tc.psum_pool(name="ps_t", bufs=3))
+        ps_t = ctx.enter_context(tc.psum_pool(name="ps_t", bufs=4))
         ps_o = ctx.enter_context(tc.psum_pool(name="ps_o", bufs=1))
 
         ident = const.tile([P, P], BF16, name="ident")
@@ -138,18 +136,11 @@ def tile_tensorproductselfinteraction_kernel(tc, node_embeddings, Z_embeddings, 
                 nc.scalar.copy(out=units[:, 3 * G : 3 * G + 3], in_=l1[:, G])
             nc.scalar.copy(out=units[:, 6:11], in_=l2)
 
-        def transpose_x0(j):
-            xt = ps_x.tile([P, 512], BF16, name="xt%d" % j, tag="xt")
-            nc.tensor.matmul(
-                out=xt[:], lhsT=xp[j][:, 0:128], rhs=ident4[:].rearrange("p q b -> p (q b)"), start=True, stop=True
-            )
-            xtd[j] = xt
-
         def product_l0(j):
             prod = ppool.tile([P, 4, 512], BF16, name="p0_%d" % j, tag="p0", align_bytes=64)
             nc.vector.tensor_tensor(
                 out=prod[:].rearrange("p g (q t) -> p g q t", t=4),
-                in0=xtd[j][:].rearrange("p (q t) -> p q t", t=4).unsqueeze(1).to_broadcast([P, 4, P, 4]),
+                in0=xtd[j].rearrange("p (q t) -> p q t", t=4).unsqueeze(1).to_broadcast([P, 4, P, 4]),
                 in1=zb[j // 2][:, j % 2, :, :].rearrange("p q (g t) -> p g q t", g=4),
                 op=MULT,
             )
@@ -177,6 +168,15 @@ def tile_tensorproductselfinteraction_kernel(tc, node_embeddings, Z_embeddings, 
                         tp[:, col : col + P], pn[j][:, r, a * 256 : (a + 1) * 256].bitcast(F32), identf[:]
                     )
             banks[(j, b)] = tp
+            if b == 5:
+                xtd[j] = tp[:, 256:512].bitcast(BF16)
+                nc.tensor.matmul(
+                    out=xtd[j],
+                    lhsT=xp[j][:, 0:128],
+                    rhs=ident4[:].rearrange("p q b -> p (q b)"),
+                    start=True,
+                    stop=True,
+                )
 
         def copy_bank(j, b, engine_copy):
             if j not in pt:
@@ -335,70 +335,70 @@ def tile_tensorproductselfinteraction_kernel(tc, node_embeddings, Z_embeddings, 
 
         permute(0)
         permute(1)
-        transpose_x0(0)
         product_units(0, range(16))
-        for b in range(3):
-            transposes(0, b)
-            copy_bank(0, b, scopy)
         permute(2)
-        product_units(1, range(0, 8))
-        quantize_units(0, 0, 4)
-        for b in range(3, 6):
+        for b in range(6):
             transposes(0, b)
-            copy_bank(0, b, scopy)
-        product_l0(0)
-        transpose_x0(1)
+            copy_bank(0, b, copy_engine(b))
+            if b == 2:
+                product_units(1, range(0, 8))
+                quantize_units(0, 0, 4)
         product_units(1, range(8, 16))
+        product_l0(0)
         quantize_units(0, 4, 4)
+        quantize_l0(0)
+        weights_l12(scopy)
+        permute(3)
         quantize_units(0, 8, 2)
         quantize_units(0, 10, 1)
-        weights_l12(scopy)
-        for g in range(4):
-            weights_l0(g, scopy)
-        quantize_l0(0)
+        for b in range(6):
+            transposes(1, b)
+            copy_bank(1, b, copy_engine(b))
+            if b == 2:
+                product_units(2, range(0, 8))
+                quantize_units(1, 0, 4)
+        product_units(2, range(8, 16))
         quantize_w12()
+        for g in range(4):
+            weights_l0(g, scopy if g % 2 == 0 else vcopy)
+        product_l0(1)
         quantize_w0(0)
+        quantize_units(1, 4, 4)
+        quantize_l0(1)
         quantize_w0(1)
 
         for i in range(NJ):
-            n1 = i + 1 < NJ
             n2 = i + 2 < NJ
-            if i > 0:
-                quantize_units(i, 8, 2)
-                quantize_units(i, 10, 1)
-            if n1:
+            n3 = i + 3 < NJ
+            if i + 1 < NJ:
+                quantize_units(i + 1, 8, 2)
+                quantize_units(i + 1, 10, 1)
+            if n2:
                 for b in range(3):
-                    transposes(i + 1, b)
-                    copy_bank(i + 1, b, copy_engine(b))
-            if n2:
-                product_units(i + 2, range(0, 4))
-            if n1:
-                product_l0(i + 1)
-            if n2:
-                product_units(i + 2, range(4, 8))
+                    transposes(i + 2, b)
+                    copy_bank(i + 2, b, copy_engine(b))
+            if n3:
+                product_units(i + 3, range(0, 8))
             for b in range(2):
                 multiply(i, b)
                 evacuate(i, b)
-            if n1:
-                quantize_l0(i + 1)
             if n2:
-                product_units(i + 2, range(8, 12))
-            if n1:
-                quantize_units(i + 1, 0, 4)
+                quantize_units(i + 2, 0, 4)
+            if n3:
+                product_units(i + 3, range(8, 16))
             if n2:
-                transpose_x0(i + 2)
-                product_units(i + 2, range(12, 16))
-            if n1:
                 for b in range(3, 6):
-                    transposes(i + 1, b)
-                    copy_bank(i + 1, b, copy_engine(b))
+                    transposes(i + 2, b)
+                    copy_bank(i + 2, b, copy_engine(b))
+                product_l0(i + 2)
             for b in range(2, 4):
                 multiply(i, b)
                 evacuate(i, b)
-            if n1:
-                quantize_units(i + 1, 4, 4)
-            if i + 3 < NJ:
-                permute(i + 3)
-            if (i + 2) % 2 == 0 and (i + 2) // 2 + 2 < NJ // 2:
-                load_z((i + 2) // 2 + 2)
+            if n2:
+                quantize_units(i + 2, 4, 4)
+                quantize_l0(i + 2)
+            if i + 4 < NJ:
+                permute(i + 4)
+            if i % 2 == 0 and i // 2 + 3 < NJ // 2:
+                load_z(i // 2 + 3)
             nc.sync.dma_start(out=out_view[i], in_=osts[i][:].rearrange("p c f -> p (c f)"))

@@ -11,6 +11,7 @@ U8 = mybir.dt.uint8
 FP8X4 = mybir.dt.float8_e4m3fn_x4
 COPY = mybir.ActivationFunctionType.Copy
 MULT = mybir.AluOpType.mult
+ADD = mybir.AluOpType.add
 
 P = 128
 NODES = 2048
@@ -121,11 +122,14 @@ def tile_tensorproductselfinteraction_kernel(tc, node_embeddings, Z_embeddings, 
         accs = {}
         osts = {}
 
+        def gpsimd_copy(out, in_):
+            nc.gpsimd.tensor_scalar(out=out, in0=in_, scalar1=1.0, scalar2=0.0, op0=MULT, op1=ADD)
+
         def permute(j):
             src = xn[j // 4][:, j % 4, :]
             dst = xpool.tile([P, FEAT], BF16, name="xp%d" % j, tag="xp")
             xp[j] = dst
-            nc.scalar.copy(
+            gpsimd_copy(
                 out=dst[:, 0:128].rearrange("p (c A e) -> p c A e", c=4, A=16, e=2),
                 in_=src[:, 0:128].rearrange("p (A c e) -> p c A e", A=16, c=4, e=2),
             )
@@ -133,8 +137,8 @@ def tile_tensorproductselfinteraction_kernel(tc, node_embeddings, Z_embeddings, 
             l1 = src[:, 128:320].rearrange("p (G m s i) -> p G i s m", G=2, m=4, s=8, i=3)
             l2 = src[:, 320:480].rearrange("p (m s i) -> p i s m", m=4, s=8, i=5)
             for G in range(2):
-                nc.scalar.copy(out=units[:, 3 * G : 3 * G + 3], in_=l1[:, G])
-            nc.scalar.copy(out=units[:, 6:11], in_=l2)
+                gpsimd_copy(out=units[:, 3 * G : 3 * G + 3], in_=l1[:, G])
+            gpsimd_copy(out=units[:, 6:11], in_=l2)
 
         def product_l0(j):
             prod = ppool.tile([P, 4, 512], BF16, name="p0_%d" % j, tag="p0", align_bytes=64)

@@ -332,10 +332,9 @@ def tile_tensorproductselfinteraction_kernel(tc, node_embeddings, Z_embeddings, 
             nc.vector.quantize_mx(out=w2c[:].bitcast(FP8X4), scales=w2s[:], in_=wg[2][:, 2048:2560])
 
         scopy = nc.scalar.copy
-        vcopy = nc.vector.tensor_copy
 
         def copy_engine(b):
-            return vcopy if b in {5} else scopy
+            return scopy
 
         permute(0)
         permute(1)
@@ -364,7 +363,7 @@ def tile_tensorproductselfinteraction_kernel(tc, node_embeddings, Z_embeddings, 
         product_units(2, range(8, 16))
         quantize_w12()
         for g in range(4):
-            weights_l0(g, scopy if g % 2 == 0 else vcopy)
+            weights_l0(g, scopy)
         product_l0(1)
         quantize_w0(0)
         quantize_units(1, 4, 4)

import math
from contextlib import ExitStack

import concourse.mybir as mybir
from concourse.masks import make_identity

BF16 = mybir.dt.bfloat16
F32 = mybir.dt.float32
U32 = mybir.dt.uint32
U8 = mybir.dt.uint8
FP8X4 = mybir.dt.float8_e4m3fn_x4
COPY = mybir.ActivationFunctionType.Copy
MULT = mybir.AluOpType.mult
ADD = mybir.AluOpType.add

P = 128
NODES = 2048
NJ = NODES // P
FEAT = 480
UNITS = 11
FLOPS = 2 * NODES * (1 * 2048 * 512 + 3 * 1024 * 256 + 5 * 512 * 128)

ALPHA0 = 1.0 / math.sqrt(2048.0)
ALPHA1 = 1.0 / math.sqrt(1024.0)
ALPHA2 = 1.0 / math.sqrt(512.0)


def tile_tensorproductselfinteraction_kernel(tc, node_embeddings, Z_embeddings, W0, W1, W2, out):
    nc = tc.nc
    x_view = node_embeddings.rearrange("(j q) f -> q j f", q=P)
    z_nat_view = Z_embeddings.rearrange("(j q) v -> q j v", q=P)
    z_view = Z_embeddings.rearrange("(k n) v -> k (n v)", k=NJ // 2)
    out_view = out.rearrange("(j q c) f -> j q (c f)", q=P, c=4)
    out_cols = out.rearrange("(j q c) f -> j q c f", q=P, c=4)
    w1_view = W1.rearrange("u v w -> (u v) w").rearrange("(G k e q a) w -> G k q e (a w)", G=2, k=2, e=2, q=64, a=2)
    w2_view = W2.rearrange("u v w -> (u v) w").rearrange("(k e q a) w -> k q e (a w)", k=2, e=2, q=64, a=2)

    with ExitStack() as ctx:
        const = ctx.enter_context(tc.tile_pool(name="const", bufs=1))
        zpool = ctx.enter_context(tc.tile_pool(name="zpool", bufs=3))
        xpool = ctx.enter_context(tc.tile_pool(name="xpool", bufs=4))
        wgpool = ctx.enter_context(tc.tile_pool(name="wgpool", bufs=2))
        npool = ctx.enter_context(tc.tile_pool(name="npool", bufs=2))
        ppool = ctx.enter_context(tc.tile_pool(name="ppool", bufs=2))
        cpool = ctx.enter_context(tc.tile_pool(name="cpool", bufs=4))
        opool = ctx.enter_context(tc.tile_pool(name="opool", bufs=3))
        ps_t = ctx.enter_context(tc.psum_pool(name="ps_t", bufs=4))
        ps_o = ctx.enter_context(tc.psum_pool(name="ps_o", bufs=1))

        ident = const.tile([P, P], BF16, name="ident")
        identf = const.tile([P, P], F32, name="identf")
        ident4 = const.tile([P, P, 4], BF16, name="ident4")
        sel0 = const.tile([P, P], BF16, name="sel0")
        selb = const.tile([P, P], BF16, name="selb")
        zn = const.tile([P, NJ, 16], BF16, name="zn")
        xn = [const.tile([P, 4, FEAT], BF16, name="xn%d" % c) for c in range(4)]
        raw0 = const.tile([P, 16, 512], BF16, name="raw0")
        raw1 = const.tile([P, 2, 2, 2, 256], BF16, name="raw1")
        raw2 = const.tile([P, 2, 2, 128], BF16, name="raw2")
        w0c = const.tile([P, 4, 512], U32, name="w0c", align_bytes=64)
        w0s = const.tile([P, 4, 512], U8, name="w0s", align_bytes=64)
        w1c = const.tile([P, 2, 256], U32, name="w1c", align_bytes=64)
        w1s = const.tile([P, 2, 256], U8, name="w1s", align_bytes=64)
        w2c = const.tile([P, 128], U32, name="w2c", align_bytes=64)
        w2s = const.tile([P, 128], U8, name="w2s", align_bytes=64)

        make_identity(nc, ident[:])
        make_identity(nc, identf[:])

        zb = {}

        def load_z(k):
            zt = zpool.tile([P, 2, P, 16], BF16, name="zb%d" % k, tag="zb")
            nc.sync.dma_start(
                out=zt[:].rearrange("p j q v -> p (j q v)"), in_=z_view[k].partition_broadcast(P)
            )
            zb[k] = zt

        def load_x(c):
            nc.sync.dma_start(out=xn[c][:], in_=x_view[:, 4 * c : 4 * c + 4, :])

        nc.sync.dma_start(out=xn[0][:, 0:1, :], in_=x_view[:, 0:1, :])
        nc.scalar.dma_start(out=zn[:], in_=z_nat_view)
        nc.sync.dma_start(out=xn[0][:, 1:4, :], in_=x_view[:, 1:4, :])
        for G in range(2):
            for k in range(2):
                nc.sync.dma_start(
                    out=raw1[64 * k : 64 * k + 64, G, :, :, :].rearrange("q e a w -> q e (a w)"), in_=w1_view[G, k]
                )
        for k in range(2):
            nc.sync.dma_start(
                out=raw2[64 * k : 64 * k + 64, :, :, :].rearrange("q e a w -> q e (a w)"), in_=w2_view[k]
            )
        load_z(0)
        for g in range(4):
            nc.sync.dma_start(out=raw0[:, 4 * g : 4 * g + 4, :], in_=W0[:, 4 * g : 4 * g + 4, :])
        load_x(1)
        load_z(1)
        load_x(2)
        load_z(2)
        load_x(3)

        nc.vector.tensor_copy(out=ident4[:], in_=ident[:].unsqueeze(2).to_broadcast([P, P, 4]))
        nc.vector.tensor_copy(
            out=sel0[:].rearrange("k (c A e) -> k c A e", c=4, A=16, e=2),
            in_=ident[:].rearrange("k (A c e) -> k c A e", A=16, c=4, e=2),
        )
        for d in range(2):
            for b in range(2):
                nc.vector.tensor_copy(
                    out=selb[:].rearrange("k (h c l b d) -> k b d h c l", h=4, c=4, l=2, b=2, d=2)[:, b, d],
                    in_=ident[:].rearrange("k (d c b h l) -> k d b h c l", d=2, c=4, b=2, h=4, l=2)[:, d, b],
                )

        xp = {}
        xtd = {}
        pn = {}
        pt = {}
        p0 = {}
        codes = {}
        banks = {}
        accs = {}
        osts = {}

        def gpsimd_copy(out, in_):
            nc.gpsimd.tensor_scalar(out=out, in0=in_, scalar1=1.0, scalar2=0.0, op0=MULT, op1=ADD)

        def permute(j):
            src = xn[j // 4][:, j % 4, :]
            dst = xpool.tile([P, FEAT], BF16, name="xp%d" % j, tag="xp")
            xp[j] = dst
            gpsimd_copy(
                out=dst[:, 0:128].rearrange("p (c A e) -> p c A e", c=4, A=16, e=2),
                in_=src[:, 0:128].rearrange("p (A c e) -> p c A e", A=16, c=4, e=2),
            )
            units = dst[:, 128:480].rearrange("p (r s m) -> p r s m", r=UNITS, s=8, m=4)
            l1 = src[:, 128:320].rearrange("p (G m s i) -> p G i s m", G=2, m=4, s=8, i=3)
            l2 = src[:, 320:480].rearrange("p (m s i) -> p i s m", m=4, s=8, i=5)
            for G in range(2):
                gpsimd_copy(out=units[:, 3 * G : 3 * G + 3], in_=l1[:, G])
            gpsimd_copy(out=units[:, 6:11], in_=l2)

        def product_l0(j):
            prod = ppool.tile([P, 4, 512], BF16, name="p0_%d" % j, tag="p0", align_bytes=64)
            nc.vector.tensor_tensor(
                out=prod[:].rearrange("p g (q t) -> p g q t", t=4),
                in0=xtd[j].rearrange("p (q t) -> p q t", t=4).unsqueeze(1).to_broadcast([P, 4, P, 4]),
                in1=zb[j // 2][:, j % 2, :, :].rearrange("p q (g t) -> p g q t", g=4),
                op=MULT,
            )
            p0[j] = prod

        def product_units(j, vs):
            if j not in pn:
                pn[j] = npool.tile([P, UNITS, 512], BF16, name="pn%d" % j, tag="pn", align_bytes=64)
            view = pn[j][:].rearrange("p r (a h c l s) -> p a h l c r s", a=2, h=4, c=4, l=2, s=8)
            for v in vs:
                nc.vector.tensor_scalar(
                    out=view[:, v % 2, v // 4, (v // 2) % 2],
                    in0=xp[j][:, 128:480].rearrange("p (r c s) -> p c r s", r=UNITS, c=4, s=8),
                    scalar1=zn[:, j, v : v + 1],
                    scalar2=None,
                    op0=MULT,
                )

        def transposes(j, b):
            tp = ps_t.tile([P, 512], F32, name="tp%d_%d" % (j, b), tag="tp")
            for r in range(2 * b, min(2 * b + 2, UNITS)):
                for a in range(2):
                    col = (2 * (r - 2 * b) + a) * P
                    nc.tensor.transpose(
                        tp[:, col : col + P], pn[j][:, r, a * 256 : (a + 1) * 256].bitcast(F32), identf[:]
                    )
            banks[(j, b)] = tp
            if b == 5:
                xtd[j] = tp[:, 256:512].bitcast(BF16)
                nc.tensor.matmul(
                    out=xtd[j],
                    lhsT=xp[j][:, 0:128],
                    rhs=ident4[:].rearrange("p q b -> p (q b)"),
                    start=True,
                    stop=True,
                )

        def copy_bank(j, b, engine_copy):
            if j not in pt:
                pt[j] = ppool.tile([P, UNITS, 512], BF16, name="pt%d" % j, tag="pt", align_bytes=64)
            n = min(2, UNITS - 2 * b)
            engine_copy(
                out=pt[j][:, 2 * b : 2 * b + n, :].bitcast(F32).rearrange("p r (n a) -> p r n a", a=2),
                in_=banks[(j, b)][:, 0 : 256 * n].rearrange("p (r a n) -> p r n a", r=n, a=2),
            )

        def code_tiles(j):
            if j not in codes:
                cj = cpool.tile([P, 15, P], U32, name="cj%d" % j, tag="cj", align_bytes=64)
                sj = cpool.tile([P, 15, P], U8, name="sj%d" % j, tag="sj", align_bytes=64)
                codes[j] = (cj, sj)
            return codes[j]

        def quantize_l0(j):
            cj, sj = code_tiles(j)
            nc.vector.quantize_mx(
                out=cj[:, 0:4, :].rearrange("p g c -> p (g c)").bitcast(FP8X4),
                scales=sj[:, 0:4, :].rearrange("p g c -> p (g c)"),
                in_=p0[j][:].rearrange("p g c -> p (g c)"),
            )

        def quantize_units(j, r0, n):
            cj, sj = code_tiles(j)
            nc.vector.quantize_mx(
                out=cj[:, 4 + r0 : 4 + r0 + n, :].rearrange("p g c -> p (g c)").bitcast(FP8X4),
                scales=sj[:, 4 + r0 : 4 + r0 + n, :].rearrange("p g c -> p (g c)"),
                in_=pt[j][:, r0 : r0 + n, :].rearrange("p g c -> p (g c)"),
            )

        def mx(acc, j, unit, rhs, rhs_scale, start, stop):
            cj, sj = codes[j]
            nc.tensor.matmul_mx(
                out=acc,
                lhsT=cj[:, unit, :].bitcast(FP8X4),
                lhsT_scale=sj[:, unit, :],
                rhs=rhs.bitcast(FP8X4),
                rhs_scale=rhs_scale,
                start=start,
                stop=stop,
            )

        def multiply(j, b):
            acc = ps_o.tile([P, 512], F32, name="o%d_%d" % (j, b), tag="o%d" % b)
            accs[(j, b)] = acc
            l0_col = 384 if b < 2 else 320
            for g in range(4):
                mx(acc[:, l0_col : l0_col + P], j, g, w0c[:, g, b * P : (b + 1) * P], w0s[:, g, b * P : (b + 1) * P], g == 0, g == 3)
            cp = b % 2
            if b < 2:
                for i in range(3):
                    for G in range(2):
                        mx(
                            acc[:, i * P : (i + 1) * P],
                            j,
                            4 + G * 3 + i,
                            w1c[:, G, cp * P : (cp + 1) * P],
                            w1s[:, G, cp * P : (cp + 1) * P],
                            G == 0,
                            G == 1,
                        )
            else:
                for i in range(5):
                    mx(
                        acc[:, i * 64 : (i + 1) * 64],
                        j,
                        10 + i,
                        w2c[:, cp * 64 : (cp + 1) * 64],
                        w2s[:, cp * 64 : (cp + 1) * 64],
                        True,
                        True,
                    )

        def evacuate(j, b):
            if j not in osts:
                osts[j] = opool.tile([P, 4, FEAT], F32, name="ost%d" % j, tag="ost")
            ost = osts[j]
            acc = accs[(j, b)]
            cp = b % 2
            l0_col = 384 if b < 2 else 320
            nc.scalar.activation(out=ost[:, b, 0:128], in_=acc[:, l0_col : l0_col + P], func=COPY, scale=ALPHA0)
            if b < 2:
                nc.scalar.activation(
                    out=ost[:, 2 * cp : 2 * cp + 2, 128:320].rearrange("p c (w i) -> p c w i", i=3),
                    in_=acc[:, 0:384].rearrange("p (i c w) -> p c w i", i=3, c=2),
                    func=COPY,
                    scale=ALPHA1,
                )
            else:
                nc.scalar.activation(
                    out=ost[:, 2 * cp : 2 * cp + 2, 320:480].rearrange("p c (w i) -> p c w i", i=5),
                    in_=acc[:, 0:320].rearrange("p (i c w) -> p c w i", i=5, c=2),
                    func=COPY,
                    scale=ALPHA2,
                )

        wg = {}
        wsn = []

        def weight_bank(sel, rhs_of_pair, width):
            wsn.append(0)
            ws = ps_t.tile([P, 1024], BF16, name="ws%d" % len(wsn), tag="tp")
            for b in range(2):
                nc.tensor.matmul(
                    out=ws[:, 0 : 4 * width].rearrange("p (w b e) -> p b w e", b=2, e=2)[:, b],
                    lhsT=sel[:],
                    rhs=rhs_of_pair(b),
                    start=True,
                    stop=True,
                )
            return ws

        def weights_l0(g, engine_copy):
            if g % 2 == 0:
                wg[g // 2] = wgpool.tile([P, 4096], BF16, name="wg0_%d" % (g // 2), tag="wg", align_bytes=64)
            for h in range(2):
                ws = weight_bank(
                    sel0,
                    lambda b: raw0[:, 4 * g + 2 * b : 4 * g + 2 * b + 2, 256 * h : 256 * h + 256].rearrange("k e w -> k w e"),
                    256,
                )
                o = (g % 2) * 2048 + h * 1024
                engine_copy(out=wg[g // 2][:, o : o + 1024], in_=ws[:])

        def quantize_w0(h):
            nc.vector.quantize_mx(
                out=w0c[:, 2 * h : 2 * h + 2, :].rearrange("p g c -> p (g c)").bitcast(FP8X4),
                scales=w0s[:, 2 * h : 2 * h + 2, :].rearrange("p g c -> p (g c)"),
                in_=wg[h][:],
            )

        def weights_l12(engine_copy):
            wg[2] = wgpool.tile([P, 4096], BF16, name="wg12", tag="wg", align_bytes=64)
            for G in range(2):
                ws = weight_bank(selb, lambda a: raw1[:, G, :, a, :].rearrange("k e w -> k w e"), 256)
                engine_copy(out=wg[2][:, G * 1024 : (G + 1) * 1024], in_=ws[:])
            ws = weight_bank(selb, lambda a: raw2[:, :, a, :].rearrange("k e w -> k w e"), 128)
            engine_copy(out=wg[2][:, 2048:2560], in_=ws[:, 0:512])

        def quantize_w12():
            nc.vector.quantize_mx(
                out=w1c[:].rearrange("p g c -> p (g c)").bitcast(FP8X4),
                scales=w1s[:].rearrange("p g c -> p (g c)"),
                in_=wg[2][:, 0:2048],
            )
            nc.vector.quantize_mx(out=w2c[:].bitcast(FP8X4), scales=w2s[:], in_=wg[2][:, 2048:2560])

        scopy = nc.scalar.copy

        def copy_engine(b):
            return scopy

        permute(0)
        permute(1)
        product_units(0, range(16))
        permute(2)
        for b in range(6):
            transposes(0, b)
            copy_bank(0, b, copy_engine(b))
            if b == 2:
                product_units(1, range(0, 8))
                quantize_units(0, 0, 4)
        product_units(1, range(8, 16))
        product_l0(0)
        quantize_units(0, 4, 4)
        quantize_l0(0)
        weights_l12(scopy)
        permute(3)
        quantize_units(0, 8, 2)
        quantize_units(0, 10, 1)
        for b in range(6):
            transposes(1, b)
            copy_bank(1, b, copy_engine(b))
            if b == 2:
                product_units(2, range(0, 8))
                quantize_units(1, 0, 4)
        product_units(2, range(8, 16))
        quantize_w12()
        for g in range(4):
            weights_l0(g, scopy)
        product_l0(1)
        quantize_w0(0)
        quantize_units(1, 4, 4)
        quantize_l0(1)
        quantize_w0(1)

        for i in range(NJ):
            n2 = i + 2 < NJ
            n3 = i + 3 < NJ
            if i + 1 < NJ:
                quantize_units(i + 1, 8, 2)
                quantize_units(i + 1, 10, 1)
            if n2:
                for b in range(3):
                    transposes(i + 2, b)
                    copy_bank(i + 2, b, copy_engine(b))
            if n3:
                product_units(i + 3, range(0, 8))
            for b in range(2):
                multiply(i, b)
                evacuate(i, b)
            if n2:
                quantize_units(i + 2, 0, 4)
            if n3:
                product_units(i + 3, range(8, 16))
            if n2:
                for b in range(3, 6):
                    transposes(i + 2, b)
                    copy_bank(i + 2, b, copy_engine(b))
                product_l0(i + 2)
            for b in range(2, 4):
                multiply(i, b)
                evacuate(i, b)
            if n2:
                quantize_units(i + 2, 4, 4)
                quantize_l0(i + 2)
            if i + 4 < NJ:
                permute(i + 4)
            if i % 2 == 0 and i // 2 + 3 < NJ // 2:
                load_z(i // 2 + 3)
            nc.sync.dma_start(out=out_view[i], in_=osts[i][:].rearrange("p c f -> p (c f)"))
